import numpy as np
import ml_dtypes


def mxq(x, axis, fmt="e4m3"):
    dtype, down = {"e4m3": (ml_dtypes.float8_e4m3fn, 7), "e5m2": (ml_dtypes.float8_e5m2, 14)}[fmt]
    v = np.moveaxis(np.asarray(x, np.float32).astype(ml_dtypes.bfloat16).astype(np.float64), axis, -1)
    blocks = v.reshape(v.shape[:-1] + (-1, 32))
    amax = np.abs(blocks).max(-1, keepdims=True)
    byte = np.maximum(np.where(amax > 0, np.frexp(amax)[1] - 1 + 127, 0) - down, 1)
    scale = np.exp2(byte - 127.0)
    codes = (blocks / scale).astype(np.float32).astype(dtype).astype(np.float64)
    return np.moveaxis((codes * scale).reshape(v.shape), -1, axis)


WIDE = False


def mx_kscale(k):
    if not WIDE:
        return np.ones(k)
    levels = np.array([10, -10, 5, -5, 0])
    a = np.random.permutation(np.resize(levels, k // 512 * 4)).reshape(k // 512, 4)
    idx = np.arange(k)
    return np.exp2(a[idx // 512, idx % 128 // 32])


BF16 = ml_dtypes.bfloat16


def bf(x):
    return np.asarray(x, np.float32).astype(BF16)


def f64(x):
    return np.asarray(x).astype(np.float64)


B, K, M, D = 2048, 256, 4, 512
KM = K * M
SX = 1.2 / D ** 0.25
TINY = 1e-10


def softmax(v, axis):
    e = np.exp(v - v.max(axis, keepdims=True))
    return e / e.sum(axis, keepdims=True)


def setup_inputs():
    s = mx_kscale(D)
    return {"x": bf(np.random.standard_normal((B, D)) * SX * s),
            "gamma_class": bf(softmax(2.0 * np.random.standard_normal((B, K)), 1)),
            "mu": bf(np.random.standard_normal((K, M, D)) * SX * s),
            "cur_var": bf(np.random.uniform(0.8, 1.2, (K, M, D)) * s * s),
            "pi": bf((0.5 + np.random.random((K, M))) / M)}


def reference(x, gamma_class, mu, cur_var, pi):
    x = f64(x)
    mu = f64(mu).reshape(KM, D)
    cur_var = f64(cur_var).reshape(KM, D)
    inv_var = 1.0 / cur_var
    maha = ((mxq(x * x, 1, "e4m3") @ mxq(inv_var, 1, "e4m3").T)
            - 2.0 * (mxq(x, 1, "e4m3") @ mxq(mu * inv_var, 1, "e4m3").T)
            + np.sum(mu * mu * inv_var, axis=-1)[None])
    log_det = np.sum(np.log(cur_var), axis=-1)
    log_lik = -0.5 * (log_det[None] + maha)
    log_joint = (np.log(f64(pi) + TINY).reshape(KM)[None] + log_lik).reshape(B, K, M)
    top = log_joint.max(2, keepdims=True)
    lse = top + np.log(np.exp(log_joint - top).sum(2, keepdims=True))
    log_r = log_joint - lse
    return f64(gamma_class)[:, :, None] * np.exp(log_r)

@@ -1,0 +1,263 @@
+from contextlib import ExitStack
+
+import concourse.masks as masks
+import concourse.mybir as mybir
+
+F32 = mybir.dt.float32
+BF16 = mybir.dt.bfloat16
+U32 = mybir.dt.uint32
+U8 = mybir.dt.uint8
+FP8X4 = mybir.dt.float8_e4m3fn_x4
+ACT = mybir.ActivationFunctionType
+ALU = mybir.AluOpType
+
+P = 128
+SAMPLES, CLASSES, MODES, FEATURES = 2048, 256, 4, 512
+PACK = 4
+ROW_TILES = SAMPLES // P
+HALVES = CLASSES // P
+CHUNK = 512
+CHUNKS = SAMPLES // CHUNK
+TILES_PER_CHUNK = CHUNK // P
+UNITS = HALVES * CHUNKS
+FIRST_BATCH = 5
+TINY = 1e-10
+
+FLOPS = 2 * 2 * SAMPLES * CLASSES * MODES * FEATURES
+
+
+def tile_dota_mix_pa_kernel(tc, x, gamma_class, mu, cur_var, pi, out):
+    nc = tc.nc
+
+    x_rows = x.rearrange("(p t) d -> p t d", t=ROW_TILES)
+    gamma_rows = gamma_class.rearrange("(p t) k -> p t k", t=ROW_TILES)
+    out_rows = out.rearrange("(p t) k m -> p t (k m)", t=ROW_TILES)
+    var_rows = cur_var.rearrange("(h p) m d -> p h (m d)", p=P)
+    mu_rows = mu.rearrange("(h p) m d -> p h (m d)", p=P)
+    pi_rows = pi.rearrange("(h p) m -> p h m", p=P)
+
+    with ExitStack() as ctx:
+        ctx.enter_context(tc.manual_schedule())
+        keep = ctx.enter_context(tc.tile_pool(name="keep", bufs=1))
+        scores = ctx.enter_context(tc.tile_pool(name="scores", bufs=UNITS))
+        work = ctx.enter_context(tc.tile_pool(name="work", bufs=2))
+        psum = ctx.enter_context(tc.psum_pool(name="psum", bufs=8))
+
+        identity = keep.tile([P, P], F32)
+        masks.make_identity(nc, identity[:])
+        tiny = keep.tile([P, 1], F32)
+        nc.vector.memset(tiny[:], TINY)
+
+        x_codes = keep.tile([P, SAMPLES], U32, align_bytes=64)
+        x_scales = keep.tile([P, SAMPLES], U8, align_bytes=64)
+        xx_codes = keep.tile([P, SAMPLES], U32, align_bytes=64)
+        xx_scales = keep.tile([P, SAMPLES], U8, align_bytes=64)
+        w_codes = keep.tile([P, 2, HALVES, MODES * P], U32, align_bytes=64)
+        w_scales = keep.tile([P, 2, HALVES, MODES * P], U8, align_bytes=64)
+        gamma_sb = keep.tile([P, ROW_TILES, CLASSES], BF16)
+        pi_sb = keep.tile([P, HALVES, MODES], BF16)
+        log_pi = keep.tile([P, HALVES * MODES], F32)
+        log_det = keep.tile([P, HALVES * MODES], F32)
+        mu_sq = keep.tile([P, HALVES * MODES], F32)
+        bias = keep.tile([P, HALVES * MODES], F32)
+        sums = keep.tile([P, UNITS, CHUNK], F32)
+
+        with tc.tile_pool(name="prep", bufs=1) as prep, tc.tile_pool(name="stage", bufs=2) as stage:
+            var_sb = prep.tile([P, HALVES, MODES * FEATURES], BF16)
+            mu_sb = prep.tile([P, HALVES, MODES * FEATURES], BF16)
+            x_sb = prep.tile([P, ROW_TILES, FEATURES], BF16)
+            nc.scalar.dma_start(out=pi_sb[:], in_=pi_rows)
+            for h in range(HALVES):
+                nc.sync.dma_start(out=var_sb[:, h, :], in_=var_rows[:, h, :])
+            for c in range(CHUNKS):
+                tiles = slice(c * TILES_PER_CHUNK, (c + 1) * TILES_PER_CHUNK)
+                nc.sync.dma_start(out=x_sb[:, tiles, :], in_=x_rows[:, tiles, :])
+            for h in range(HALVES):
+                nc.sync.dma_start(out=mu_sb[:, h, :], in_=mu_rows[:, h, :])
+            nc.sync.dma_start(out=gamma_sb[:], in_=gamma_rows)
+
+            iv = prep.tile([P, HALVES, MODES * FEATURES], F32)
+            mu_iv = prep.tile([P, HALVES, MODES * FEATURES], F32)
+            nc.scalar.activation(
+                out=log_pi[:], in_=pi_sb[:].rearrange("p h m -> p (h m)"), func=ACT.Ln, bias=tiny[:]
+            )
+            for h in range(HALVES):
+                for m in range(MODES):
+                    cols = slice(m * FEATURES, (m + 1) * FEATURES)
+                    nc.scalar.activation(
+                        out=iv[:, h, cols],
+                        in_=var_sb[:, h, cols],
+                        func=ACT.Ln,
+                        accum_out=log_det[:, h * MODES + m : h * MODES + m + 1],
+                    )
+
+            def prepare_samples(c):
+                x_words = x_sb[:].bitcast(F32)
+                grouped = stage.tile([P, CHUNK * PACK], BF16, align_bytes=64)
+                grouped_words = grouped[:].bitcast(F32).rearrange("p (b u) -> p b u", u=2)
+                for half in range(2):
+                    bank = psum.tile([P, 512], F32)
+                    for u in range(2):
+                        for j in range(2):
+                            t = c * TILES_PER_CHUNK + 2 * half + j
+                            nc.tensor.transpose(
+                                bank[:, (2 * u + j) * P : (2 * u + j + 1) * P],
+                                x_words[:, t, u * P : (u + 1) * P],
+                                identity[:],
+                            )
+                    nc.vector.tensor_copy(
+                        out=grouped_words[:, half * 256 : (half + 1) * 256, :],
+                        in_=bank[:].rearrange("p (u b) -> p b u", u=2),
+                    )
+                squared = stage.tile([P, CHUNK * PACK], BF16, align_bytes=64)
+                nc.vector.tensor_tensor(out=squared[:], in0=grouped[:], in1=grouped[:], op=ALU.mult)
+                cols = slice(c * CHUNK, (c + 1) * CHUNK)
+                nc.vector.quantize_mx(
+                    out=x_codes[:, cols].bitcast(FP8X4), scales=x_scales[:, cols], in_=grouped[:]
+                )
+                nc.vector.quantize_mx(
+                    out=xx_codes[:, cols].bitcast(FP8X4), scales=xx_scales[:, cols], in_=squared[:]
+                )
+
+            prepare_samples(0)
+            prepare_samples(1)
+
+            for h in range(HALVES):
+                for m in range(MODES):
+                    cols = slice(m * FEATURES, (m + 1) * FEATURES)
+                    nc.scalar.activation(out=iv[:, h, cols], in_=iv[:, h, cols], func=ACT.Exp, scale=-1.0)
+                    nc.vector.tensor_tensor(
+                        out=mu_iv[:, h, cols], in0=mu_sb[:, h, cols], in1=iv[:, h, cols], op=ALU.mult
+                    )
+
+            prepare_samples(2)
+            prepare_samples(3)
+
+            for h in range(HALVES):
+                for m in range(MODES):
+                    cols = slice(m * FEATURES, (m + 1) * FEATURES)
+                    product = stage.tile([P, FEATURES], F32)
+                    nc.vector.scalar_tensor_tensor(
+                        out=product[:],
+                        in0=mu_sb[:, h, cols],
+                        scalar=1.0,
+                        in1=mu_iv[:, h, cols],
+                        op0=ALU.mult,
+                        op1=ALU.mult,
+                        accum_out=mu_sq[:, h * MODES + m : h * MODES + m + 1],
+                    )
+            nc.vector.tensor_tensor(out=bias[:], in0=log_det[:], in1=mu_sq[:], op=ALU.add)
+            nc.vector.scalar_tensor_tensor(
+                out=bias[:], in0=bias[:], scalar=-0.5, in1=log_pi[:], op0=ALU.mult, op1=ALU.add
+            )
+
+            for h in range(HALVES):
+                for a, (source, factor) in enumerate(((iv, -0.5), (mu_iv, 1.0))):
+                    grouped_w = stage.tile([P, MODES * P * PACK], BF16, align_bytes=64)
+                    grouped_view = grouped_w[:].rearrange("p (m k t) -> p m k t", m=MODES, t=PACK)
+                    for m in range(MODES):
+                        cols = slice(m * FEATURES, (m + 1) * FEATURES)
+                        by_value = source[:, h, cols].rearrange("p (u q e) -> p u e q", u=2, e=2)
+                        bank = psum.tile([P, 512], F32)
+                        for u in range(2):
+                            for e in range(2):
+                                t = 2 * u + e
+                                nc.tensor.transpose(bank[:, t * P : (t + 1) * P], by_value[:, u, e, :], identity[:])
+                        nc.scalar.activation(
+                            out=grouped_view[:, m, :, :],
+                            in_=bank[:].rearrange("p (t k) -> p k t", t=PACK),
+                            func=ACT.Copy,
+                            scale=factor,
+                        )
+                    nc.vector.quantize_mx(
+                        out=w_codes[:, a, h, :].bitcast(FP8X4), scales=w_scales[:, a, h, :], in_=grouped_w[:]
+                    )
+
+        def reciprocals(first, last):
+            span = sums[:, first:last, :]
+            nc.scalar.activation(out=span, in_=span, func=ACT.Ln)
+            nc.scalar.activation(out=span, in_=span, func=ACT.Exp, scale=-1.0)
+
+        exps = []
+        for unit in range(UNITS):
+            h, c = divmod(unit, CHUNKS)
+            cols = slice(c * CHUNK, (c + 1) * CHUNK)
+            joint = []
+            for m in range(MODES):
+                classes = slice(m * P, (m + 1) * P)
+                bank = psum.tile([P, 512], F32)
+                nc.tensor.matmul_mx(
+                    out=bank[:],
+                    lhsT=w_codes[:, 0, h, classes].bitcast(FP8X4),
+                    lhsT_scale=w_scales[:, 0, h, classes],
+                    rhs=xx_codes[:, cols].bitcast(FP8X4),
+                    rhs_scale=xx_scales[:, cols],
+                    start=True,
+                    stop=False,
+                )
+                nc.tensor.matmul_mx(
+                    out=bank[:],
+                    lhsT=w_codes[:, 1, h, classes].bitcast(FP8X4),
+                    lhsT_scale=w_scales[:, 1, h, classes],
+                    rhs=x_codes[:, cols].bitcast(FP8X4),
+                    rhs_scale=x_scales[:, cols],
+                    start=False,
+                    stop=True,
+                )
+                joint.append(bank)
+            top = work.tile([P, CHUNK], F32)
+            nc.vector.tensor_scalar_add(out=top[:], in0=joint[0][:], scalar1=bias[:, h * MODES : h * MODES + 1])
+            for m in range(1, MODES):
+                nc.vector.scalar_tensor_tensor(
+                    out=top[:],
+                    in0=joint[m][:],
+                    scalar=bias[:, h * MODES + m : h * MODES + m + 1],
+                    in1=top[:],
+                    op0=ALU.add,
+                    op1=ALU.max,
+                )
+            e = scores.tile([P, MODES, CHUNK], F32, name="e")
+            exps.append(e)
+            for m in range(MODES):
+                nc.vector.tensor_tensor(out=e[:, m, :], in0=joint[m][:], in1=top[:], op=ALU.subtract)
+                nc.scalar.activation(
+                    out=e[:, m, :], in_=e[:, m, :], func=ACT.Exp, bias=bias[:, h * MODES + m : h * MODES + m + 1]
+                )
+            pair = work.tile([P, 2, CHUNK], F32)
+            nc.gpsimd.tensor_tensor(out=pair[:], in0=e[:, 0:2, :], in1=e[:, 2:4, :], op=ALU.add)
+            nc.gpsimd.tensor_tensor(out=sums[:, unit, :], in0=pair[:, 0, :], in1=pair[:, 1, :], op=ALU.add)
+            if unit == FIRST_BATCH:
+                reciprocals(0, FIRST_BATCH)
+        reciprocals(FIRST_BATCH, UNITS)
+
+        with tc.tile_pool(name="finish", bufs=2) as finish:
+            for unit in range(UNITS):
+                h, c = divmod(unit, CHUNKS)
+                tiles = slice(c * TILES_PER_CHUNK, (c + 1) * TILES_PER_CHUNK)
+                e = exps[unit]
+                bank = psum.tile([P, 512], F32)
+                for s in range(TILES_PER_CHUNK):
+                    block = slice(s * P, (s + 1) * P)
+                    nc.tensor.transpose(bank[:, block], sums[:, unit, block], identity[:])
+                weight = finish.tile([P, TILES_PER_CHUNK, P], F32)
+                nc.vector.tensor_tensor(
+                    out=weight[:],
+                    in0=bank[:].rearrange("p (s k) -> p s k", s=TILES_PER_CHUNK),
+                    in1=gamma_sb[:, tiles, h * P : (h + 1) * P],
+                    op=ALU.mult,
+                )
+                result = finish.tile([P, TILES_PER_CHUNK, P * MODES], F32)
+                for s in range(TILES_PER_CHUNK):
+                    block = slice(s * P, (s + 1) * P)
+                    bank = psum.tile([P, 512], F32)
+                    for m in range(MODES):
+                        nc.tensor.transpose(bank[:, m * P : (m + 1) * P], e[:, m, block], identity[:])
+                    nc.vector.tensor_tensor(
+                        out=result[:, s, :].rearrange("p (k m) -> p k m", m=MODES),
+                        in0=bank[:].rearrange("p (m k) -> p k m", m=MODES),
+                        in1=weight[:, s, :].unsqueeze(2).to_broadcast([P, P, MODES]),
+                        op=ALU.mult,
+                    )
+                nc.sync.dma_start(
+                    out=out_rows[:, tiles, h * P * MODES : (h + 1) * P * MODES], in_=result[:]
+                )

@@ -20,7 +20,7 @@ CHUNK = 512
 CHUNKS = SAMPLES // CHUNK
 TILES_PER_CHUNK = CHUNK // P
 UNITS = HALVES * CHUNKS
-FIRST_BATCH = 5
+FIRST_ROUND = 5
 TINY = 1e-10
 
 FLOPS = 2 * 2 * SAMPLES * CLASSES * MODES * FEATURES
@@ -40,7 +40,7 @@ def tile_dota_mix_pa_kernel(tc, x, gamma_class, mu, cur_var, pi, out):
         ctx.enter_context(tc.manual_schedule())
         keep = ctx.enter_context(tc.tile_pool(name="keep", bufs=1))
         scores = ctx.enter_context(tc.tile_pool(name="scores", bufs=UNITS))
-        work = ctx.enter_context(tc.tile_pool(name="work", bufs=2))
+        work = ctx.enter_context(tc.tile_pool(name="work", bufs=3))
         psum = ctx.enter_context(tc.psum_pool(name="psum", bufs=8))
 
         identity = keep.tile([P, P], F32)
@@ -54,7 +54,6 @@ def tile_dota_mix_pa_kernel(tc, x, gamma_class, mu, cur_var, pi, out):
         xx_scales = keep.tile([P, SAMPLES], U8, align_bytes=64)
         w_codes = keep.tile([P, 2, HALVES, MODES * P], U32, align_bytes=64)
         w_scales = keep.tile([P, 2, HALVES, MODES * P], U8, align_bytes=64)
-        gamma_sb = keep.tile([P, ROW_TILES, CLASSES], BF16)
         pi_sb = keep.tile([P, HALVES, MODES], BF16)
         log_pi = keep.tile([P, HALVES * MODES], F32)
         log_det = keep.tile([P, HALVES * MODES], F32)
@@ -62,22 +61,75 @@ def tile_dota_mix_pa_kernel(tc, x, gamma_class, mu, cur_var, pi, out):
         bias = keep.tile([P, HALVES * MODES], F32)
         sums = keep.tile([P, UNITS, CHUNK], F32)
 
+        joint = {}
+        tops = {}
+        exps = {}
+
+        def bias_of(unit, m):
+            column = (unit // CHUNKS) * MODES + m
+            return bias[:, column : column + 1]
+
+        def multiply(unit, m):
+            h, c = divmod(unit, CHUNKS)
+            cols = slice(c * CHUNK, (c + 1) * CHUNK)
+            classes = slice(m * P, (m + 1) * P)
+            bank = psum.tile([P, 512], F32)
+            nc.tensor.matmul_mx(
+                out=bank[:],
+                lhsT=w_codes[:, 0, h, classes].bitcast(FP8X4),
+                lhsT_scale=w_scales[:, 0, h, classes],
+                rhs=xx_codes[:, cols].bitcast(FP8X4),
+                rhs_scale=xx_scales[:, cols],
+                start=True,
+                stop=False,
+            )
+            nc.tensor.matmul_mx(
+                out=bank[:],
+                lhsT=w_codes[:, 1, h, classes].bitcast(FP8X4),
+                lhsT_scale=w_scales[:, 1, h, classes],
+                rhs=x_codes[:, cols].bitcast(FP8X4),
+                rhs_scale=x_scales[:, cols],
+                start=False,
+                stop=True,
+            )
+            joint[(unit, m)] = bank
+
+        def start_maximum(unit):
+            top = work.tile([P, CHUNK], F32)
+            nc.scalar.activation(out=top[:], in_=joint[(unit, 0)][:], func=ACT.Identity, bias=bias_of(unit, 0))
+            tops[unit] = top
+
+        def raise_maximum(unit, m):
+            nc.vector.scalar_tensor_tensor(
+                out=tops[unit][:],
+                in0=joint[(unit, m)][:],
+                scalar=bias_of(unit, m),
+                in1=tops[unit][:],
+                op0=ALU.add,
+                op1=ALU.max,
+            )
+
         with tc.tile_pool(name="prep", bufs=1) as prep, tc.tile_pool(name="stage", bufs=2) as stage:
             var_sb = prep.tile([P, HALVES, MODES * FEATURES], BF16)
             mu_sb = prep.tile([P, HALVES, MODES * FEATURES], BF16)
             x_sb = prep.tile([P, ROW_TILES, FEATURES], BF16)
             nc.scalar.dma_start(out=pi_sb[:], in_=pi_rows)
-            for h in range(HALVES):
-                nc.sync.dma_start(out=var_sb[:, h, :], in_=var_rows[:, h, :])
-            for c in range(CHUNKS):
+            def load_samples(c):
                 tiles = slice(c * TILES_PER_CHUNK, (c + 1) * TILES_PER_CHUNK)
                 nc.sync.dma_start(out=x_sb[:, tiles, :], in_=x_rows[:, tiles, :])
+
+            load_samples(0)
+            for h in range(HALVES):
+                nc.sync.dma_start(out=var_sb[:, h, :], in_=var_rows[:, h, :])
+            for c in range(1, CHUNKS):
+                load_samples(c)
             for h in range(HALVES):
                 nc.sync.dma_start(out=mu_sb[:, h, :], in_=mu_rows[:, h, :])
-            nc.sync.dma_start(out=gamma_sb[:], in_=gamma_rows)
 
             iv = prep.tile([P, HALVES, MODES * FEATURES], F32)
             mu_iv = prep.tile([P, HALVES, MODES * FEATURES], F32)
+            warm = prep.tile([P, 1], F32)
+            nc.scalar.activation(out=warm[:], in_=tiny[:], func=ACT.Ln)
             nc.scalar.activation(
                 out=log_pi[:], in_=pi_sb[:].rearrange("p h m -> p (h m)"), func=ACT.Ln, bias=tiny[:]
             )
@@ -119,10 +171,7 @@ def tile_dota_mix_pa_kernel(tc, x, gamma_class, mu, cur_var, pi, out):
                     out=xx_codes[:, cols].bitcast(FP8X4), scales=xx_scales[:, cols], in_=squared[:]
                 )
 
-            prepare_samples(0)
-            prepare_samples(1)
-
-            for h in range(HALVES):
+            def invert(h):
                 for m in range(MODES):
                     cols = slice(m * FEATURES, (m + 1) * FEATURES)
                     nc.scalar.activation(out=iv[:, h, cols], in_=iv[:, h, cols], func=ACT.Exp, scale=-1.0)
@@ -130,10 +179,27 @@ def tile_dota_mix_pa_kernel(tc, x, gamma_class, mu, cur_var, pi, out):
                         out=mu_iv[:, h, cols], in0=mu_sb[:, h, cols], in1=iv[:, h, cols], op=ALU.mult
                     )
 
-            prepare_samples(2)
-            prepare_samples(3)
+            def transpose_weights(source, factor, h):
+                grouped_w = stage.tile([P, MODES * P * PACK], BF16, align_bytes=64, bufs=4)
+                grouped_view = grouped_w[:].rearrange("p (m k t) -> p m k t", m=MODES, t=PACK)
+                for m in range(MODES):
+                    cols = slice(m * FEATURES, (m + 1) * FEATURES)
+                    by_value = source[:, h, cols].rearrange("p (u q e) -> p u e q", u=2, e=2)
+                    bank = psum.tile([P, 512], F32)
+                    for u in range(2):
+                        for odd in range(2):
+                            t = 2 * u + odd
+                            nc.tensor.transpose(bank[:, t * P : (t + 1) * P], by_value[:, u, odd, :], identity[:])
+                    nc.scalar.activation(
+                        out=grouped_view[:, m, :, :],
+                        in_=bank[:].rearrange("p (t k) -> p k t", t=PACK),
+                        func=ACT.Copy,
+                        scale=factor,
+                    )
+                return grouped_w
 
-            for h in range(HALVES):
+            def finish_half(h, grouped_iv, grouped_mu_iv):
+                modes = slice(h * MODES, (h + 1) * MODES)
                 for m in range(MODES):
                     cols = slice(m * FEATURES, (m + 1) * FEATURES)
                     product = stage.tile([P, FEATURES], F32)
@@ -146,95 +212,70 @@ def tile_dota_mix_pa_kernel(tc, x, gamma_class, mu, cur_var, pi, out):
                         op1=ALU.mult,
                         accum_out=mu_sq[:, h * MODES + m : h * MODES + m + 1],
                     )
-            nc.vector.tensor_tensor(out=bias[:], in0=log_det[:], in1=mu_sq[:], op=ALU.add)
-            nc.vector.scalar_tensor_tensor(
-                out=bias[:], in0=bias[:], scalar=-0.5, in1=log_pi[:], op0=ALU.mult, op1=ALU.add
-            )
-
-            for h in range(HALVES):
-                for a, (source, factor) in enumerate(((iv, -0.5), (mu_iv, 1.0))):
-                    grouped_w = stage.tile([P, MODES * P * PACK], BF16, align_bytes=64)
-                    grouped_view = grouped_w[:].rearrange("p (m k t) -> p m k t", m=MODES, t=PACK)
-                    for m in range(MODES):
-                        cols = slice(m * FEATURES, (m + 1) * FEATURES)
-                        by_value = source[:, h, cols].rearrange("p (u q e) -> p u e q", u=2, e=2)
-                        bank = psum.tile([P, 512], F32)
-                        for u in range(2):
-                            for e in range(2):
-                                t = 2 * u + e
-                                nc.tensor.transpose(bank[:, t * P : (t + 1) * P], by_value[:, u, e, :], identity[:])
-                        nc.scalar.activation(
-                            out=grouped_view[:, m, :, :],
-                            in_=bank[:].rearrange("p (t k) -> p k t", t=PACK),
-                            func=ACT.Copy,
-                            scale=factor,
-                        )
+                nc.vector.tensor_tensor(out=bias[:, modes], in0=log_det[:, modes], in1=mu_sq[:, modes], op=ALU.add)
+                nc.vector.scalar_tensor_tensor(
+                    out=bias[:, modes], in0=bias[:, modes], scalar=-0.5, in1=log_pi[:, modes], op0=ALU.mult, op1=ALU.add
+                )
+                for a, grouped_w in enumerate((grouped_iv, grouped_mu_iv)):
                     nc.vector.quantize_mx(
                         out=w_codes[:, a, h, :].bitcast(FP8X4), scales=w_scales[:, a, h, :], in_=grouped_w[:]
                     )
 
-        def reciprocals(first, last):
-            span = sums[:, first:last, :]
-            nc.scalar.activation(out=span, in_=span, func=ACT.Ln)
-            nc.scalar.activation(out=span, in_=span, func=ACT.Exp, scale=-1.0)
+            prepare_samples(0)
+            prepare_samples(1)
+            invert(0)
+            invert(1)
+            prepare_samples(2)
+            prepare_samples(3)
+            grouped = [(transpose_weights(iv, -0.5, h), transpose_weights(mu_iv, 1.0, h)) for h in range(HALVES)]
+            finish_half(0, grouped[0][0], grouped[0][1])
+            for unit in range(2):
+                for m in range(MODES):
+                    multiply(unit, m)
+                start_maximum(unit)
+            finish_half(1, grouped[1][0], grouped[1][1])
 
-        exps = []
+        def reciprocals(first, last):
+            for unit in range(first, last):
+                nc.scalar.activation(out=sums[:, unit, :], in_=sums[:, unit, :], func=ACT.Ln)
+            for unit in range(first, last):
+                nc.scalar.activation(out=sums[:, unit, :], in_=sums[:, unit, :], func=ACT.Exp, scale=-1.0)
+
+        for m in range(1, MODES):
+            raise_maximum(0, m)
         for unit in range(UNITS):
-            h, c = divmod(unit, CHUNKS)
-            cols = slice(c * CHUNK, (c + 1) * CHUNK)
-            joint = []
+            expd = scores.tile([P, MODES, CHUNK], F32)
+            exps[unit] = expd
             for m in range(MODES):
-                classes = slice(m * P, (m + 1) * P)
-                bank = psum.tile([P, 512], F32)
-                nc.tensor.matmul_mx(
-                    out=bank[:],
-                    lhsT=w_codes[:, 0, h, classes].bitcast(FP8X4),
-                    lhsT_scale=w_scales[:, 0, h, classes],
-                    rhs=xx_codes[:, cols].bitcast(FP8X4),
-                    rhs_scale=xx_scales[:, cols],
-                    start=True,
-                    stop=False,
+                nc.vector.tensor_tensor(
+                    out=expd[:, m, :], in0=joint[(unit, m)][:], in1=tops[unit][:], op=ALU.subtract
                 )
-                nc.tensor.matmul_mx(
-                    out=bank[:],
-                    lhsT=w_codes[:, 1, h, classes].bitcast(FP8X4),
-                    lhsT_scale=w_scales[:, 1, h, classes],
-                    rhs=x_codes[:, cols].bitcast(FP8X4),
-                    rhs_scale=x_scales[:, cols],
-                    start=False,
-                    stop=True,
-                )
-                joint.append(bank)
-            top = work.tile([P, CHUNK], F32)
-            nc.vector.tensor_scalar_add(out=top[:], in0=joint[0][:], scalar1=bias[:, h * MODES : h * MODES + 1])
-            for m in range(1, MODES):
-                nc.vector.scalar_tensor_tensor(
-                    out=top[:],
-                    in0=joint[m][:],
-                    scalar=bias[:, h * MODES + m : h * MODES + m + 1],
-                    in1=top[:],
-                    op0=ALU.add,
-                    op1=ALU.max,
-                )
-            e = scores.tile([P, MODES, CHUNK], F32, name="e")
-            exps.append(e)
-            for m in range(MODES):
-                nc.vector.tensor_tensor(out=e[:, m, :], in0=joint[m][:], in1=top[:], op=ALU.subtract)
-                nc.scalar.activation(
-                    out=e[:, m, :], in_=e[:, m, :], func=ACT.Exp, bias=bias[:, h * MODES + m : h * MODES + m + 1]
-                )
-            pair = work.tile([P, 2, CHUNK], F32)
-            nc.gpsimd.tensor_tensor(out=pair[:], in0=e[:, 0:2, :], in1=e[:, 2:4, :], op=ALU.add)
-            nc.gpsimd.tensor_tensor(out=sums[:, unit, :], in0=pair[:, 0, :], in1=pair[:, 1, :], op=ALU.add)
-            if unit == FIRST_BATCH:
-                reciprocals(0, FIRST_BATCH)
-        reciprocals(FIRST_BATCH, UNITS)
+                nc.scalar.activation(out=expd[:, m, :], in_=expd[:, m, :], func=ACT.Exp, bias=bias_of(unit, m))
+                if m > 0:
+                    nc.gpsimd.tensor_tensor(
+                        out=sums[:, unit, :],
+                        in0=expd[:, 0, :] if m == 1 else sums[:, unit, :],
+                        in1=expd[:, m, :],
+                        op=ALU.add,
+                    )
+                if unit + 2 < UNITS:
+                    multiply(unit + 2, m)
+                    if m == 0:
+                        start_maximum(unit + 2)
+                if unit + 1 < UNITS and m + 1 < MODES:
+                    raise_maximum(unit + 1, m + 1)
+                if unit == FIRST_ROUND and m == 2:
+                    reciprocals(0, FIRST_ROUND)
+        reciprocals(FIRST_ROUND, UNITS)
 
         with tc.tile_pool(name="finish", bufs=2) as finish:
-            for unit in range(UNITS):
+            gamma_sb = finish.tile([P, ROW_TILES, CLASSES], BF16, bufs=1)
+            nc.sync.dma_start(out=gamma_sb[:], in_=gamma_rows)
+            weights = {}
+
+            def make_weight(unit):
                 h, c = divmod(unit, CHUNKS)
                 tiles = slice(c * TILES_PER_CHUNK, (c + 1) * TILES_PER_CHUNK)
-                e = exps[unit]
                 bank = psum.tile([P, 512], F32)
                 for s in range(TILES_PER_CHUNK):
                     block = slice(s * P, (s + 1) * P)
@@ -246,18 +287,23 @@ def tile_dota_mix_pa_kernel(tc, x, gamma_class, mu, cur_var, pi, out):
                     in1=gamma_sb[:, tiles, h * P : (h + 1) * P],
                     op=ALU.mult,
                 )
-                result = finish.tile([P, TILES_PER_CHUNK, P * MODES], F32)
+                weights[unit] = weight
+
+            for unit in range(UNITS):
+                h, c = divmod(unit, CHUNKS)
+                make_weight(unit)
                 for s in range(TILES_PER_CHUNK):
                     block = slice(s * P, (s + 1) * P)
                     bank = psum.tile([P, 512], F32)
                     for m in range(MODES):
-                        nc.tensor.transpose(bank[:, m * P : (m + 1) * P], e[:, m, block], identity[:])
+                        nc.tensor.transpose(bank[:, m * P : (m + 1) * P], exps[unit][:, m, block], identity[:])
+                    result = finish.tile([P, P * MODES], F32, bufs=4)
                     nc.vector.tensor_tensor(
-                        out=result[:, s, :].rearrange("p (k m) -> p k m", m=MODES),
+                        out=result[:].rearrange("p (k m) -> p k m", m=MODES),
                         in0=bank[:].rearrange("p (m k) -> p k m", m=MODES),
-                        in1=weight[:, s, :].unsqueeze(2).to_broadcast([P, P, MODES]),
+                        in1=weights[unit][:, s, :].unsqueeze(2).to_broadcast([P, P, MODES]),
                         op=ALU.mult,
                     )
-                nc.sync.dma_start(
-                    out=out_rows[:, tiles, h * P * MODES : (h + 1) * P * MODES], in_=result[:]
-                )
+                    nc.sync.dma_start(
+                        out=out_rows[:, c * TILES_PER_CHUNK + s, h * P * MODES : (h + 1) * P * MODES], in_=result[:]
+                    )

@@ -14,12 +14,18 @@ ALU = mybir.AluOpType
 P = 128
 SAMPLES, CLASSES, MODES, FEATURES = 2048, 256, 4, 512
 PACK = 4
+PSUM_BANKS = 8
+BANK = 512
 ROW_TILES = SAMPLES // P
 HALVES = CLASSES // P
-CHUNK = 512
+CHUNK = BANK
 CHUNKS = SAMPLES // CHUNK
 TILES_PER_CHUNK = CHUNK // P
+WORD_HALVES = FEATURES // 2 // P
+TILES_PER_BANK = BANK // (WORD_HALVES * P)
+SAMPLES_PER_BANK = TILES_PER_BANK * P
 UNITS = HALVES * CHUNKS
+OTHER_MODES = MODES - 1
 FIRST_ROUND = 5
 TINY = 1e-10
 
@@ -41,7 +47,7 @@ def tile_dota_mix_pa_kernel(tc, x, gamma_class, mu, cur_var, pi, out):
         keep = ctx.enter_context(tc.tile_pool(name="keep", bufs=1))
         scores = ctx.enter_context(tc.tile_pool(name="scores", bufs=UNITS))
         work = ctx.enter_context(tc.tile_pool(name="work", bufs=3))
-        psum = ctx.enter_context(tc.psum_pool(name="psum", bufs=8))
+        psum = ctx.enter_context(tc.psum_pool(name="psum", bufs=PSUM_BANKS))
 
         identity = keep.tile([P, P], F32)
         masks.make_identity(nc, identity[:])
@@ -59,6 +65,7 @@ def tile_dota_mix_pa_kernel(tc, x, gamma_class, mu, cur_var, pi, out):
         log_det = keep.tile([P, HALVES * MODES], F32)
         mu_sq = keep.tile([P, HALVES * MODES], F32)
         bias = keep.tile([P, HALVES * MODES], F32)
+        bias_gap = keep.tile([P, HALVES * MODES], F32)
         sums = keep.tile([P, UNITS, CHUNK], F32)
 
         joint = {}
@@ -67,53 +74,54 @@ def tile_dota_mix_pa_kernel(tc, x, gamma_class, mu, cur_var, pi, out):
 
         def bias_of(unit, m):
             column = (unit // CHUNKS) * MODES + m
-            return bias[:, column : column + 1]
+            return bias_gap[:, column : column + 1]
 
         def multiply(unit, m):
             h, c = divmod(unit, CHUNKS)
             cols = slice(c * CHUNK, (c + 1) * CHUNK)
-            classes = slice(m * P, (m + 1) * P)
-            bank = psum.tile([P, 512], F32)
-            nc.tensor.matmul_mx(
-                out=bank[:],
-                lhsT=w_codes[:, 0, h, classes].bitcast(FP8X4),
-                lhsT_scale=w_scales[:, 0, h, classes],
-                rhs=xx_codes[:, cols].bitcast(FP8X4),
-                rhs_scale=xx_scales[:, cols],
-                start=True,
-                stop=False,
-            )
-            nc.tensor.matmul_mx(
-                out=bank[:],
-                lhsT=w_codes[:, 1, h, classes].bitcast(FP8X4),
-                lhsT_scale=w_scales[:, 1, h, classes],
-                rhs=x_codes[:, cols].bitcast(FP8X4),
-                rhs_scale=x_scales[:, cols],
-                start=False,
-                stop=True,
-            )
+            bank = psum.tile([P, BANK], F32)
+            passes = [(mode, a) for mode in (m, 0) for a in range(2)]
+            for i, (mode, a) in enumerate(passes):
+                classes = slice(mode * P, (mode + 1) * P)
+                moving_codes, moving_scales = ((xx_codes, xx_scales), (x_codes, x_scales))[a]
+                nc.tensor.matmul_mx(
+                    out=bank[:],
+                    lhsT=w_codes[:, a, h, classes].bitcast(FP8X4),
+                    lhsT_scale=w_scales[:, a, h, classes],
+                    rhs=moving_codes[:, cols].bitcast(FP8X4),
+                    rhs_scale=moving_scales[:, cols],
+                    start=(i == 0),
+                    stop=(i == len(passes) - 1),
+                )
             joint[(unit, m)] = bank
 
-        def start_maximum(unit):
-            top = work.tile([P, CHUNK], F32)
-            nc.scalar.activation(out=top[:], in_=joint[(unit, 0)][:], func=ACT.Identity, bias=bias_of(unit, 0))
-            tops[unit] = top
+        def multiply_nth(n):
+            if n < UNITS * OTHER_MODES:
+                multiply(n // OTHER_MODES, n % OTHER_MODES + 1)
 
         def raise_maximum(unit, m):
-            nc.vector.scalar_tensor_tensor(
-                out=tops[unit][:],
-                in0=joint[(unit, m)][:],
-                scalar=bias_of(unit, m),
-                in1=tops[unit][:],
-                op0=ALU.add,
-                op1=ALU.max,
-            )
+            if m == 1:
+                top = work.tile([P, CHUNK], F32)
+                tops[unit] = top
+                nc.vector.tensor_scalar(
+                    out=top[:], in0=joint[(unit, m)][:], scalar1=bias_of(unit, m), scalar2=0.0, op0=ALU.add, op1=ALU.max
+                )
+            else:
+                nc.vector.scalar_tensor_tensor(
+                    out=tops[unit][:],
+                    in0=joint[(unit, m)][:],
+                    scalar=bias_of(unit, m),
+                    in1=tops[unit][:],
+                    op0=ALU.add,
+                    op1=ALU.max,
+                )
 
         with tc.tile_pool(name="prep", bufs=1) as prep, tc.tile_pool(name="stage", bufs=2) as stage:
             var_sb = prep.tile([P, HALVES, MODES * FEATURES], BF16)
             mu_sb = prep.tile([P, HALVES, MODES * FEATURES], BF16)
             x_sb = prep.tile([P, ROW_TILES, FEATURES], BF16)
             nc.scalar.dma_start(out=pi_sb[:], in_=pi_rows)
+
             def load_samples(c):
                 tiles = slice(c * TILES_PER_CHUNK, (c + 1) * TILES_PER_CHUNK)
                 nc.sync.dma_start(out=x_sb[:, tiles, :], in_=x_rows[:, tiles, :])
@@ -146,20 +154,20 @@ def tile_dota_mix_pa_kernel(tc, x, gamma_class, mu, cur_var, pi, out):
             def prepare_samples(c):
                 x_words = x_sb[:].bitcast(F32)
                 grouped = stage.tile([P, CHUNK * PACK], BF16, align_bytes=64)
-                grouped_words = grouped[:].bitcast(F32).rearrange("p (b u) -> p b u", u=2)
-                for half in range(2):
-                    bank = psum.tile([P, 512], F32)
-                    for u in range(2):
-                        for j in range(2):
-                            t = c * TILES_PER_CHUNK + 2 * half + j
+                grouped_words = grouped[:].bitcast(F32).rearrange("p (b u) -> p b u", u=WORD_HALVES)
+                for half in range(CHUNK // SAMPLES_PER_BANK):
+                    bank = psum.tile([P, BANK], F32)
+                    for u in range(WORD_HALVES):
+                        for j in range(TILES_PER_BANK):
+                            t = c * TILES_PER_CHUNK + TILES_PER_BANK * half + j
                             nc.tensor.transpose(
-                                bank[:, (2 * u + j) * P : (2 * u + j + 1) * P],
+                                bank[:, (TILES_PER_BANK * u + j) * P : (TILES_PER_BANK * u + j + 1) * P],
                                 x_words[:, t, u * P : (u + 1) * P],
                                 identity[:],
                             )
                     nc.vector.tensor_copy(
-                        out=grouped_words[:, half * 256 : (half + 1) * 256, :],
-                        in_=bank[:].rearrange("p (u b) -> p b u", u=2),
+                        out=grouped_words[:, half * SAMPLES_PER_BANK : (half + 1) * SAMPLES_PER_BANK, :],
+                        in_=bank[:].rearrange("p (u b) -> p b u", u=WORD_HALVES),
                     )
                 squared = stage.tile([P, CHUNK * PACK], BF16, align_bytes=64)
                 nc.vector.tensor_tensor(out=squared[:], in0=grouped[:], in1=grouped[:], op=ALU.mult)
@@ -180,13 +188,13 @@ def tile_dota_mix_pa_kernel(tc, x, gamma_class, mu, cur_var, pi, out):
                     )
 
             def transpose_weights(source, factor, h):
-                grouped_w = stage.tile([P, MODES * P * PACK], BF16, align_bytes=64, bufs=4)
+                grouped_w = stage.tile([P, MODES * P * PACK], BF16, align_bytes=64, bufs=2 * HALVES)
                 grouped_view = grouped_w[:].rearrange("p (m k t) -> p m k t", m=MODES, t=PACK)
                 for m in range(MODES):
                     cols = slice(m * FEATURES, (m + 1) * FEATURES)
-                    by_value = source[:, h, cols].rearrange("p (u q e) -> p u e q", u=2, e=2)
-                    bank = psum.tile([P, 512], F32)
-                    for u in range(2):
+                    by_value = source[:, h, cols].rearrange("p (u q e) -> p u e q", u=WORD_HALVES, e=2)
+                    bank = psum.tile([P, BANK], F32)
+                    for u in range(WORD_HALVES):
                         for odd in range(2):
                             t = 2 * u + odd
                             nc.tensor.transpose(bank[:, t * P : (t + 1) * P], by_value[:, u, odd, :], identity[:])
@@ -194,7 +202,7 @@ def tile_dota_mix_pa_kernel(tc, x, gamma_class, mu, cur_var, pi, out):
                         out=grouped_view[:, m, :, :],
                         in_=bank[:].rearrange("p (t k) -> p k t", t=PACK),
                         func=ACT.Copy,
-                        scale=factor,
+                        scale=factor if m > 0 else -factor,
                     )
                 return grouped_w
 
@@ -216,6 +224,9 @@ def tile_dota_mix_pa_kernel(tc, x, gamma_class, mu, cur_var, pi, out):
                 nc.vector.scalar_tensor_tensor(
                     out=bias[:, modes], in0=bias[:, modes], scalar=-0.5, in1=log_pi[:, modes], op0=ALU.mult, op1=ALU.add
                 )
+                nc.vector.tensor_scalar_sub(
+                    out=bias_gap[:, modes], in0=bias[:, modes], scalar1=bias[:, h * MODES : h * MODES + 1]
+                )
                 for a, grouped_w in enumerate((grouped_iv, grouped_mu_iv)):
                     nc.vector.quantize_mx(
                         out=w_codes[:, a, h, :].bitcast(FP8X4), scales=w_scales[:, a, h, :], in_=grouped_w[:]
@@ -229,10 +240,8 @@ def tile_dota_mix_pa_kernel(tc, x, gamma_class, mu, cur_var, pi, out):
             prepare_samples(3)
             grouped = [(transpose_weights(iv, -0.5, h), transpose_weights(mu_iv, 1.0, h)) for h in range(HALVES)]
             finish_half(0, grouped[0][0], grouped[0][1])
-            for unit in range(2):
-                for m in range(MODES):
-                    multiply(unit, m)
-                start_maximum(unit)
+            for n in range(PSUM_BANKS):
+                multiply_nth(n)
             finish_half(1, grouped[1][0], grouped[1][1])
 
         def reciprocals(first, last):
@@ -246,24 +255,21 @@ def tile_dota_mix_pa_kernel(tc, x, gamma_class, mu, cur_var, pi, out):
         for unit in range(UNITS):
             expd = scores.tile([P, MODES, CHUNK], F32)
             exps[unit] = expd
-            for m in range(MODES):
+            nc.scalar.activation(out=expd[:, 0, :], in_=tops[unit][:], func=ACT.Exp, scale=-1.0)
+            for m in range(1, MODES):
+                if unit + 1 < UNITS:
+                    raise_maximum(unit + 1, m)
                 nc.vector.tensor_tensor(
                     out=expd[:, m, :], in0=joint[(unit, m)][:], in1=tops[unit][:], op=ALU.subtract
                 )
+                multiply_nth(unit * OTHER_MODES + m - 1 + PSUM_BANKS)
                 nc.scalar.activation(out=expd[:, m, :], in_=expd[:, m, :], func=ACT.Exp, bias=bias_of(unit, m))
-                if m > 0:
-                    nc.gpsimd.tensor_tensor(
-                        out=sums[:, unit, :],
-                        in0=expd[:, 0, :] if m == 1 else sums[:, unit, :],
-                        in1=expd[:, m, :],
-                        op=ALU.add,
-                    )
-                if unit + 2 < UNITS:
-                    multiply(unit + 2, m)
-                    if m == 0:
-                        start_maximum(unit + 2)
-                if unit + 1 < UNITS and m + 1 < MODES:
-                    raise_maximum(unit + 1, m + 1)
+                nc.gpsimd.tensor_tensor(
+                    out=sums[:, unit, :],
+                    in0=expd[:, 0, :] if m == 1 else sums[:, unit, :],
+                    in1=expd[:, m, :],
+                    op=ALU.add,
+                )
                 if unit == FIRST_ROUND and m == 2:
                     reciprocals(0, FIRST_ROUND)
         reciprocals(FIRST_ROUND, UNITS)
@@ -276,7 +282,7 @@ def tile_dota_mix_pa_kernel(tc, x, gamma_class, mu, cur_var, pi, out):
             def make_weight(unit):
                 h, c = divmod(unit, CHUNKS)
                 tiles = slice(c * TILES_PER_CHUNK, (c + 1) * TILES_PER_CHUNK)
-                bank = psum.tile([P, 512], F32)
+                bank = psum.tile([P, BANK], F32)
                 for s in range(TILES_PER_CHUNK):
                     block = slice(s * P, (s + 1) * P)
                     nc.tensor.transpose(bank[:, block], sums[:, unit, block], identity[:])
@@ -294,10 +300,10 @@ def tile_dota_mix_pa_kernel(tc, x, gamma_class, mu, cur_var, pi, out):
                 make_weight(unit)
                 for s in range(TILES_PER_CHUNK):
                     block = slice(s * P, (s + 1) * P)
-                    bank = psum.tile([P, 512], F32)
+                    bank = psum.tile([P, BANK], F32)
                     for m in range(MODES):
                         nc.tensor.transpose(bank[:, m * P : (m + 1) * P], exps[unit][:, m, block], identity[:])
-                    result = finish.tile([P, P * MODES], F32, bufs=4)
+                    result = finish.tile([P, P * MODES], F32, bufs=TILES_PER_CHUNK)
                     nc.vector.tensor_tensor(
                         out=result[:].rearrange("p (k m) -> p k m", m=MODES),
                         in0=bank[:].rearrange("p (m k) -> p k m", m=MODES),

@@ -26,10 +26,26 @@ TILES_PER_BANK = BANK // (WORD_HALVES * P)
 SAMPLES_PER_BANK = TILES_PER_BANK * P
 UNITS = HALVES * CHUNKS
 OTHER_MODES = MODES - 1
+JOINT_BANKS = 6
+TURN_BANKS = PSUM_BANKS - JOINT_BANKS
 FIRST_ROUND = 5
 TINY = 1e-10
 
 FLOPS = 2 * 2 * SAMPLES * CLASSES * MODES * FEATURES
+
+
+MU_IV_BUFS = 1
+SCORE_BUFS = 8
+SUM_BUFS = 7
+WEIGHT_BUFS = 8
+RESULT_BUFS = 8
+EVENTS = {(0,1,0): "P0", (0,2,0): "P1", (0,2,1): "P2", (0,3,0): "P3", (0,3,1): "S3", (0,3,2): "X3 Y3", (1,1,0): "Q0", (1,2,0): "Q1 B0", (4,1,0): "T0", (4,2,0): "T1", (4,3,2): "L0 T2 L1 T3 L2 L3 I0 I1 I2 I3", (6,2,1): "W0", (6,3,0): "W1", (6,3,1): "W2", (7,1,0): "W3"}
+TAIL = "F6 U60 F1 T4 L4 U61 F1 U62 F1 U63 L6 T5 L5 F1 T7 L7 F6 I4 W4 I5 W5 I6 W6 I7 W7"
+ON_VECTOR = (6,7)
+TENSOR_SUMS = (6,)
+WEIGH_ON_VECTOR = (0,1,2,3,4)
+LATE_EXP = ()
+ON_GPSIMD = ()
 
 
 def tile_dota_mix_pa_kernel(tc, x, gamma_class, mu, cur_var, pi, out):
@@ -45,9 +61,11 @@ def tile_dota_mix_pa_kernel(tc, x, gamma_class, mu, cur_var, pi, out):
     with ExitStack() as ctx:
         ctx.enter_context(tc.manual_schedule())
         keep = ctx.enter_context(tc.tile_pool(name="keep", bufs=1))
-        scores = ctx.enter_context(tc.tile_pool(name="scores", bufs=UNITS))
+        stage = ctx.enter_context(tc.tile_pool(name="stage", bufs=2))
+        scores = ctx.enter_context(tc.tile_pool(name="scores", bufs=SCORE_BUFS))
         work = ctx.enter_context(tc.tile_pool(name="work", bufs=3))
-        psum = ctx.enter_context(tc.psum_pool(name="psum", bufs=PSUM_BANKS))
+        joint_pool = ctx.enter_context(tc.psum_pool(name="joint", bufs=JOINT_BANKS))
+        turn_pool = ctx.enter_context(tc.psum_pool(name="turn", bufs=TURN_BANKS))
 
         identity = keep.tile([P, P], F32)
         masks.make_identity(nc, identity[:])
@@ -66,11 +84,157 @@ def tile_dota_mix_pa_kernel(tc, x, gamma_class, mu, cur_var, pi, out):
         mu_sq = keep.tile([P, HALVES * MODES], F32)
         bias = keep.tile([P, HALVES * MODES], F32)
         bias_gap = keep.tile([P, HALVES * MODES], F32)
-        sums = keep.tile([P, UNITS, CHUNK], F32)
+        var_sb = keep.tile([P, HALVES, MODES * FEATURES], BF16)
+        mu_sb = keep.tile([P, HALVES, MODES * FEATURES], BF16)
+        x_sb = keep.tile([P, ROW_TILES, FEATURES], BF16)
+        gamma_sb = keep.tile([P, ROW_TILES, CLASSES], BF16)
+        iv = keep.tile([P, HALVES, MODES * FEATURES], F32)
+
+        nc.scalar.dma_start(out=pi_sb[:], in_=pi_rows)
+
+        def load_samples(c):
+            tiles = slice(c * TILES_PER_CHUNK, (c + 1) * TILES_PER_CHUNK)
+            nc.sync.dma_start(out=x_sb[:, tiles, :], in_=x_rows[:, tiles, :])
+
+        nc.sync.dma_start(out=var_sb[:, 0, :], in_=var_rows[:, 0, :])
+        load_samples(0)
+        nc.sync.dma_start(out=var_sb[:, 1, :], in_=var_rows[:, 1, :])
+        load_samples(1)
+        nc.sync.dma_start(out=mu_sb[:, 0, :], in_=mu_rows[:, 0, :])
+        load_samples(2)
+        nc.sync.dma_start(out=mu_sb[:, 1, :], in_=mu_rows[:, 1, :])
+        load_samples(3)
+        nc.sync.dma_start(out=gamma_sb[:], in_=gamma_rows)
+
+        grouped = {}
+        squared = {}
+        grouped_w = {}
+        mu_iv = {}
+
+        def take_logs(h):
+            for m in range(MODES):
+                cols = slice(m * FEATURES, (m + 1) * FEATURES)
+                nc.scalar.activation(
+                    out=iv[:, h, cols],
+                    in_=var_sb[:, h, cols],
+                    func=ACT.Ln,
+                    accum_out=log_det[:, h * MODES + m : h * MODES + m + 1],
+                )
+
+        def lift_samples(c, half, copy, pool):
+            x_words = x_sb[:].bitcast(F32)
+            if half == 0:
+                grouped_x = stage.tile([P, CHUNK * PACK], BF16, align_bytes=64)
+                grouped[c] = grouped_x
+            words = grouped[c][:].bitcast(F32).rearrange("p (b u) -> p b u", u=WORD_HALVES)
+            bank = pool.tile([P, BANK], F32)
+            for u in range(WORD_HALVES):
+                for j in range(TILES_PER_BANK):
+                    t = c * TILES_PER_CHUNK + TILES_PER_BANK * half + j
+                    nc.tensor.transpose(
+                        bank[:, (TILES_PER_BANK * u + j) * P : (TILES_PER_BANK * u + j + 1) * P],
+                        x_words[:, t, u * P : (u + 1) * P],
+                        identity[:],
+                    )
+            lifted[(c, half)] = (bank, words)
+            if copy:
+                copy_samples(c, half, copy)
+
+        lifted = {}
+
+        def copy_samples(c, half, copy):
+            bank, words = lifted[(c, half)]
+            copy(
+                out=words[:, half * SAMPLES_PER_BANK : (half + 1) * SAMPLES_PER_BANK, :],
+                in_=bank[:].rearrange("p (u b) -> p b u", u=WORD_HALVES),
+            )
+
+        def square(c):
+            squared_x = stage.tile([P, CHUNK * PACK], BF16, align_bytes=64)
+            nc.vector.tensor_tensor(out=squared_x[:], in0=grouped[c][:], in1=grouped[c][:], op=ALU.mult)
+            squared[c] = squared_x
+
+        def quantise_samples(c, codes, scales, source):
+            cols = slice(c * CHUNK, (c + 1) * CHUNK)
+            nc.vector.quantize_mx(out=codes[:, cols].bitcast(FP8X4), scales=scales[:, cols], in_=source[c][:])
+
+        def quantise_x(c):
+            quantise_samples(c, x_codes, x_scales, grouped)
+
+        def quantise_xx(c):
+            quantise_samples(c, xx_codes, xx_scales, squared)
+
+        def invert(h, m):
+            cols = slice(m * FEATURES, (m + 1) * FEATURES)
+            nc.scalar.activation(out=iv[:, h, cols], in_=iv[:, h, cols], func=ACT.Exp, scale=-1.0)
+
+        def weigh_mu(h, m):
+            cols = slice(m * FEATURES, (m + 1) * FEATURES)
+            if m == 0:
+                mu_iv_h = stage.tile([P, MODES * FEATURES], F32, bufs=MU_IV_BUFS)
+                mu_iv[h] = mu_iv_h
+            nc.vector.tensor_tensor(out=mu_iv[h][:, cols], in0=mu_sb[:, h, cols], in1=iv[:, h, cols], op=ALU.mult)
+
+        def lift_weights(a, h, m, pool):
+            if m == 0:
+                grouped_wa = stage.tile([P, MODES * P * PACK], BF16, align_bytes=64, bufs=2)
+                grouped_w[(a, h)] = grouped_wa
+            view = grouped_w[(a, h)][:].rearrange("p (m k t) -> p m k t", m=MODES, t=PACK)
+            cols = slice(m * FEATURES, (m + 1) * FEATURES)
+            source = mu_iv[h][:, cols] if a == 1 else iv[:, h, cols]
+            factor = 1.0 if a == 1 else -0.5
+            by_value = source.rearrange("p (u q e) -> p u e q", u=WORD_HALVES, e=2)
+            bank = pool.tile([P, BANK], F32)
+            for u in range(WORD_HALVES):
+                for odd in range(2):
+                    t = 2 * u + odd
+                    nc.tensor.transpose(bank[:, t * P : (t + 1) * P], by_value[:, u, odd, :], identity[:])
+            nc.scalar.activation(
+                out=view[:, m, :, :],
+                in_=bank[:].rearrange("p (t k) -> p k t", t=PACK),
+                func=ACT.Copy,
+                scale=factor if m > 0 else -factor,
+            )
+
+        def quantise_weights(a, h):
+            nc.vector.quantize_mx(
+                out=w_codes[:, a, h, :].bitcast(FP8X4), scales=w_scales[:, a, h, :], in_=grouped_w[(a, h)][:]
+            )
+
+        def sum_mu_sq(h, m):
+            cols = slice(m * FEATURES, (m + 1) * FEATURES)
+            nc.vector.scalar_tensor_tensor(
+                out=mu_iv[h][:, cols],
+                in0=mu_sb[:, h, cols],
+                scalar=1.0,
+                in1=mu_iv[h][:, cols],
+                op0=ALU.mult,
+                op1=ALU.mult,
+                accum_out=mu_sq[:, h * MODES + m : h * MODES + m + 1],
+            )
+
+        def finish_bias(h):
+            modes = slice(h * MODES, (h + 1) * MODES)
+            nc.gpsimd.tensor_tensor(out=bias[:, modes], in0=log_det[:, modes], in1=mu_sq[:, modes], op=ALU.add)
+            nc.gpsimd.tensor_scalar(
+                out=bias[:, modes], in0=bias[:, modes], scalar1=-0.5, scalar2=0.0, op0=ALU.mult, op1=ALU.add
+            )
+            nc.gpsimd.tensor_tensor(out=bias[:, modes], in0=bias[:, modes], in1=log_pi[:, modes], op=ALU.add)
+            nc.gpsimd.tensor_scalar(
+                out=bias_gap[:, modes],
+                in0=bias[:, modes],
+                scalar1=bias[:, h * MODES : h * MODES + 1],
+                scalar2=0.0,
+                op0=ALU.subtract,
+                op1=ALU.add,
+            )
 
         joint = {}
         tops = {}
         exps = {}
+        sums = {}
+        turned = {}
+        weights = {}
 
         def bias_of(unit, m):
             column = (unit // CHUNKS) * MODES + m
@@ -79,7 +243,7 @@ def tile_dota_mix_pa_kernel(tc, x, gamma_class, mu, cur_var, pi, out):
         def multiply(unit, m):
             h, c = divmod(unit, CHUNKS)
             cols = slice(c * CHUNK, (c + 1) * CHUNK)
-            bank = psum.tile([P, BANK], F32)
+            bank = joint_pool.tile([P, BANK], F32)
             passes = [(mode, a) for mode in (m, 0) for a in range(2)]
             for i, (mode, a) in enumerate(passes):
                 classes = slice(mode * P, (mode + 1) * P)
@@ -99,217 +263,251 @@ def tile_dota_mix_pa_kernel(tc, x, gamma_class, mu, cur_var, pi, out):
             if n < UNITS * OTHER_MODES:
                 multiply(n // OTHER_MODES, n % OTHER_MODES + 1)
 
-        def raise_maximum(unit, m):
-            if m == 1:
-                top = work.tile([P, CHUNK], F32)
-                tops[unit] = top
-                nc.vector.tensor_scalar(
-                    out=top[:], in0=joint[(unit, m)][:], scalar1=bias_of(unit, m), scalar2=0.0, op0=ALU.add, op1=ALU.max
-                )
+        def start_maximum(unit, on_scalar):
+            top = work.tile([P, CHUNK], F32)
+            tops[unit] = top
+            if on_scalar:
+                nc.scalar.activation(out=top[:], in_=joint[(unit, 1)][:], func=ACT.Relu, bias=bias_of(unit, 1))
             else:
-                nc.vector.scalar_tensor_tensor(
-                    out=tops[unit][:],
-                    in0=joint[(unit, m)][:],
-                    scalar=bias_of(unit, m),
-                    in1=tops[unit][:],
-                    op0=ALU.add,
-                    op1=ALU.max,
+                nc.vector.tensor_scalar(
+                    out=top[:], in0=joint[(unit, 1)][:], scalar1=bias_of(unit, 1), scalar2=0.0, op0=ALU.add, op1=ALU.max
                 )
 
-        with tc.tile_pool(name="prep", bufs=1) as prep, tc.tile_pool(name="stage", bufs=2) as stage:
-            var_sb = prep.tile([P, HALVES, MODES * FEATURES], BF16)
-            mu_sb = prep.tile([P, HALVES, MODES * FEATURES], BF16)
-            x_sb = prep.tile([P, ROW_TILES, FEATURES], BF16)
-            nc.scalar.dma_start(out=pi_sb[:], in_=pi_rows)
-
-            def load_samples(c):
-                tiles = slice(c * TILES_PER_CHUNK, (c + 1) * TILES_PER_CHUNK)
-                nc.sync.dma_start(out=x_sb[:, tiles, :], in_=x_rows[:, tiles, :])
-
-            load_samples(0)
-            for h in range(HALVES):
-                nc.sync.dma_start(out=var_sb[:, h, :], in_=var_rows[:, h, :])
-            for c in range(1, CHUNKS):
-                load_samples(c)
-            for h in range(HALVES):
-                nc.sync.dma_start(out=mu_sb[:, h, :], in_=mu_rows[:, h, :])
-
-            iv = prep.tile([P, HALVES, MODES * FEATURES], F32)
-            mu_iv = prep.tile([P, HALVES, MODES * FEATURES], F32)
-            warm = prep.tile([P, 1], F32)
-            nc.scalar.activation(out=warm[:], in_=tiny[:], func=ACT.Ln)
-            nc.scalar.activation(
-                out=log_pi[:], in_=pi_sb[:].rearrange("p h m -> p (h m)"), func=ACT.Ln, bias=tiny[:]
+        def raise_maximum(unit, m):
+            nc.vector.scalar_tensor_tensor(
+                out=tops[unit][:],
+                in0=joint[(unit, m)][:],
+                scalar=bias_of(unit, m),
+                in1=tops[unit][:],
+                op0=ALU.add,
+                op1=ALU.max,
             )
-            for h in range(HALVES):
-                for m in range(MODES):
-                    cols = slice(m * FEATURES, (m + 1) * FEATURES)
-                    nc.scalar.activation(
-                        out=iv[:, h, cols],
-                        in_=var_sb[:, h, cols],
-                        func=ACT.Ln,
-                        accum_out=log_det[:, h * MODES + m : h * MODES + m + 1],
-                    )
 
-            def prepare_samples(c):
-                x_words = x_sb[:].bitcast(F32)
-                grouped = stage.tile([P, CHUNK * PACK], BF16, align_bytes=64)
-                grouped_words = grouped[:].bitcast(F32).rearrange("p (b u) -> p b u", u=WORD_HALVES)
-                for half in range(CHUNK // SAMPLES_PER_BANK):
-                    bank = psum.tile([P, BANK], F32)
-                    for u in range(WORD_HALVES):
-                        for j in range(TILES_PER_BANK):
-                            t = c * TILES_PER_CHUNK + TILES_PER_BANK * half + j
-                            nc.tensor.transpose(
-                                bank[:, (TILES_PER_BANK * u + j) * P : (TILES_PER_BANK * u + j + 1) * P],
-                                x_words[:, t, u * P : (u + 1) * P],
-                                identity[:],
-                            )
-                    nc.vector.tensor_copy(
-                        out=grouped_words[:, half * SAMPLES_PER_BANK : (half + 1) * SAMPLES_PER_BANK, :],
-                        in_=bank[:].rearrange("p (u b) -> p b u", u=WORD_HALVES),
-                    )
-                squared = stage.tile([P, CHUNK * PACK], BF16, align_bytes=64)
-                nc.vector.tensor_tensor(out=squared[:], in0=grouped[:], in1=grouped[:], op=ALU.mult)
-                cols = slice(c * CHUNK, (c + 1) * CHUNK)
-                nc.vector.quantize_mx(
-                    out=x_codes[:, cols].bitcast(FP8X4), scales=x_scales[:, cols], in_=grouped[:]
-                )
-                nc.vector.quantize_mx(
-                    out=xx_codes[:, cols].bitcast(FP8X4), scales=xx_scales[:, cols], in_=squared[:]
-                )
-
-            def invert(h):
-                for m in range(MODES):
-                    cols = slice(m * FEATURES, (m + 1) * FEATURES)
-                    nc.scalar.activation(out=iv[:, h, cols], in_=iv[:, h, cols], func=ACT.Exp, scale=-1.0)
-                    nc.vector.tensor_tensor(
-                        out=mu_iv[:, h, cols], in0=mu_sb[:, h, cols], in1=iv[:, h, cols], op=ALU.mult
-                    )
-
-            def transpose_weights(source, factor, h):
-                grouped_w = stage.tile([P, MODES * P * PACK], BF16, align_bytes=64, bufs=2 * HALVES)
-                grouped_view = grouped_w[:].rearrange("p (m k t) -> p m k t", m=MODES, t=PACK)
-                for m in range(MODES):
-                    cols = slice(m * FEATURES, (m + 1) * FEATURES)
-                    by_value = source[:, h, cols].rearrange("p (u q e) -> p u e q", u=WORD_HALVES, e=2)
-                    bank = psum.tile([P, BANK], F32)
-                    for u in range(WORD_HALVES):
-                        for odd in range(2):
-                            t = 2 * u + odd
-                            nc.tensor.transpose(bank[:, t * P : (t + 1) * P], by_value[:, u, odd, :], identity[:])
-                    nc.scalar.activation(
-                        out=grouped_view[:, m, :, :],
-                        in_=bank[:].rearrange("p (t k) -> p k t", t=PACK),
-                        func=ACT.Copy,
-                        scale=factor if m > 0 else -factor,
-                    )
-                return grouped_w
-
-            def finish_half(h, grouped_iv, grouped_mu_iv):
-                modes = slice(h * MODES, (h + 1) * MODES)
-                for m in range(MODES):
-                    cols = slice(m * FEATURES, (m + 1) * FEATURES)
-                    product = stage.tile([P, FEATURES], F32)
-                    nc.vector.scalar_tensor_tensor(
-                        out=product[:],
-                        in0=mu_sb[:, h, cols],
-                        scalar=1.0,
-                        in1=mu_iv[:, h, cols],
-                        op0=ALU.mult,
-                        op1=ALU.mult,
-                        accum_out=mu_sq[:, h * MODES + m : h * MODES + m + 1],
-                    )
-                nc.vector.tensor_tensor(out=bias[:, modes], in0=log_det[:, modes], in1=mu_sq[:, modes], op=ALU.add)
-                nc.vector.scalar_tensor_tensor(
-                    out=bias[:, modes], in0=bias[:, modes], scalar=-0.5, in1=log_pi[:, modes], op0=ALU.mult, op1=ALU.add
-                )
-                nc.vector.tensor_scalar_sub(
-                    out=bias_gap[:, modes], in0=bias[:, modes], scalar1=bias[:, h * MODES : h * MODES + 1]
-                )
-                for a, grouped_w in enumerate((grouped_iv, grouped_mu_iv)):
-                    nc.vector.quantize_mx(
-                        out=w_codes[:, a, h, :].bitcast(FP8X4), scales=w_scales[:, a, h, :], in_=grouped_w[:]
-                    )
-
-            prepare_samples(0)
-            prepare_samples(1)
-            invert(0)
-            invert(1)
-            prepare_samples(2)
-            prepare_samples(3)
-            grouped = [(transpose_weights(iv, -0.5, h), transpose_weights(mu_iv, 1.0, h)) for h in range(HALVES)]
-            finish_half(0, grouped[0][0], grouped[0][1])
-            for n in range(PSUM_BANKS):
-                multiply_nth(n)
-            finish_half(1, grouped[1][0], grouped[1][1])
-
-        def reciprocals(first, last):
-            for unit in range(first, last):
-                nc.scalar.activation(out=sums[:, unit, :], in_=sums[:, unit, :], func=ACT.Ln)
-            for unit in range(first, last):
-                nc.scalar.activation(out=sums[:, unit, :], in_=sums[:, unit, :], func=ACT.Exp, scale=-1.0)
-
-        for m in range(1, MODES):
-            raise_maximum(0, m)
-        for unit in range(UNITS):
-            expd = scores.tile([P, MODES, CHUNK], F32)
-            exps[unit] = expd
+        def exp_first(unit):
+            if unit not in exps:
+                expd = scores.tile([P, MODES, CHUNK], F32)
+                exps[unit] = expd
+            expd = exps[unit]
             nc.scalar.activation(out=expd[:, 0, :], in_=tops[unit][:], func=ACT.Exp, scale=-1.0)
-            for m in range(1, MODES):
-                if unit + 1 < UNITS:
-                    raise_maximum(unit + 1, m)
-                nc.vector.tensor_tensor(
-                    out=expd[:, m, :], in0=joint[(unit, m)][:], in1=tops[unit][:], op=ALU.subtract
-                )
-                multiply_nth(unit * OTHER_MODES + m - 1 + PSUM_BANKS)
-                nc.scalar.activation(out=expd[:, m, :], in_=expd[:, m, :], func=ACT.Exp, bias=bias_of(unit, m))
-                nc.gpsimd.tensor_tensor(
-                    out=sums[:, unit, :],
-                    in0=expd[:, 0, :] if m == 1 else sums[:, unit, :],
-                    in1=expd[:, m, :],
-                    op=ALU.add,
-                )
-                if unit == FIRST_ROUND and m == 2:
-                    reciprocals(0, FIRST_ROUND)
-        reciprocals(FIRST_ROUND, UNITS)
 
-        with tc.tile_pool(name="finish", bufs=2) as finish:
-            gamma_sb = finish.tile([P, ROW_TILES, CLASSES], BF16, bufs=1)
-            nc.sync.dma_start(out=gamma_sb[:], in_=gamma_rows)
-            weights = {}
+        def subtract(unit, m):
+            expd = exps[unit]
+            nc.vector.tensor_tensor(out=expd[:, m, :], in0=joint[(unit, m)][:], in1=tops[unit][:], op=ALU.subtract)
 
-            def make_weight(unit):
-                h, c = divmod(unit, CHUNKS)
-                tiles = slice(c * TILES_PER_CHUNK, (c + 1) * TILES_PER_CHUNK)
-                bank = psum.tile([P, BANK], F32)
-                for s in range(TILES_PER_CHUNK):
-                    block = slice(s * P, (s + 1) * P)
-                    nc.tensor.transpose(bank[:, block], sums[:, unit, block], identity[:])
-                weight = finish.tile([P, TILES_PER_CHUNK, P], F32)
-                nc.vector.tensor_tensor(
-                    out=weight[:],
-                    in0=bank[:].rearrange("p (s k) -> p s k", s=TILES_PER_CHUNK),
-                    in1=gamma_sb[:, tiles, h * P : (h + 1) * P],
-                    op=ALU.mult,
-                )
-                weights[unit] = weight
+        def exp_mode(unit, m):
+            expd = exps[unit]
+            nc.scalar.activation(out=expd[:, m, :], in_=expd[:, m, :], func=ACT.Exp, bias=bias_of(unit, m))
 
-            for unit in range(UNITS):
-                h, c = divmod(unit, CHUNKS)
-                make_weight(unit)
-                for s in range(TILES_PER_CHUNK):
-                    block = slice(s * P, (s + 1) * P)
-                    bank = psum.tile([P, BANK], F32)
+        def add_mode(unit, m):
+            if unit in TENSOR_SUMS:
+                return
+            expd = exps[unit]
+            if m == 1:
+                total = work.tile([P, CHUNK], F32, bufs=SUM_BUFS)
+                sums[unit] = total
+            total = sums[unit]
+            nc.gpsimd.tensor_tensor(
+                out=total[:], in0=expd[:, 0, :] if m == 1 else total[:], in1=expd[:, m, :], op=ALU.add
+            )
+
+        def turn_sum(unit, blocks=range(TILES_PER_CHUNK)):
+            if unit not in turned:
+                pool = joint_pool if unit in TENSOR_SUMS else turn_pool
+                bank = pool.tile([P, BANK], F32)
+                turned[unit] = bank
+            bank = turned[unit]
+            for s in blocks:
+                block = slice(s * P, (s + 1) * P)
+                if unit in TENSOR_SUMS:
                     for m in range(MODES):
-                        nc.tensor.transpose(bank[:, m * P : (m + 1) * P], exps[unit][:, m, block], identity[:])
-                    result = finish.tile([P, P * MODES], F32, bufs=TILES_PER_CHUNK)
-                    nc.vector.tensor_tensor(
-                        out=result[:].rearrange("p (k m) -> p k m", m=MODES),
-                        in0=bank[:].rearrange("p (m k) -> p k m", m=MODES),
-                        in1=weights[unit][:, s, :].unsqueeze(2).to_broadcast([P, P, MODES]),
-                        op=ALU.mult,
-                    )
-                    nc.sync.dma_start(
-                        out=out_rows[:, c * TILES_PER_CHUNK + s, h * P * MODES : (h + 1) * P * MODES], in_=result[:]
-                    )
+                        nc.tensor.matmul(
+                            bank[:, block],
+                            lhsT=exps[unit][:, m, block],
+                            rhs=identity[:],
+                            start=(m == 0),
+                            stop=(m == MODES - 1),
+                        )
+                else:
+                    nc.tensor.transpose(bank[:, block], sums[unit][:, block], identity[:])
+
+        def log_sum(unit):
+            bank = turned[unit]
+            weight = work.tile([P, TILES_PER_CHUNK, P], F32, bufs=WEIGHT_BUFS)
+            nc.scalar.activation(
+                out=weight[:], in_=bank[:].rearrange("p (s k) -> p s k", s=TILES_PER_CHUNK), func=ACT.Ln
+            )
+            weights[unit] = weight
+
+        def invert_sum(unit):
+            nc.scalar.activation(out=weights[unit][:], in_=weights[unit][:], func=ACT.Exp, scale=-1.0)
+
+        def weigh(unit):
+            ready.append(unit)
+            h, c = divmod(unit, CHUNKS)
+            tiles = slice(c * TILES_PER_CHUNK, (c + 1) * TILES_PER_CHUNK)
+            engine = nc.vector if unit in WEIGH_ON_VECTOR else nc.gpsimd
+            engine.tensor_tensor(
+                out=weights[unit][:], in0=weights[unit][:], in1=gamma_sb[:, tiles, h * P : (h + 1) * P], op=ALU.mult
+            )
+
+        def finish(unit, s):
+            h, c = divmod(unit, CHUNKS)
+            block = slice(s * P, (s + 1) * P)
+            pool = joint_pool if (UNITS - 1, MODES - 1) in joint else turn_pool
+            bank = pool.tile([P, BANK], F32)
+            for m in range(MODES):
+                nc.tensor.transpose(bank[:, m * P : (m + 1) * P], exps[unit][:, m, block], identity[:])
+            result = work.tile([P, P * MODES], F32, bufs=RESULT_BUFS)
+            source = bank
+            engine = nc.vector
+            if (unit, s) in ON_GPSIMD:
+                plain = work.tile([P, P * MODES], F32, bufs=2)
+                nc.scalar.copy(out=plain[:], in_=bank[:])
+                source = plain
+                engine = nc.gpsimd
+            engine.tensor_tensor(
+                out=result[:].rearrange("p (k m) -> p k m", m=MODES),
+                in0=source[:].rearrange("p (m k) -> p k m", m=MODES),
+                in1=weights[unit][:, s, :].unsqueeze(2).to_broadcast([P, P, MODES]),
+                op=ALU.mult,
+            )
+            nc.sync.dma_start(
+                out=out_rows[:, c * TILES_PER_CHUNK + s, h * P * MODES : (h + 1) * P * MODES], in_=result[:]
+            )
+
+        ready = []
+        pending = [(unit, s) for unit in range(UNITS) for s in range(TILES_PER_CHUNK)]
+
+        def finish_some(count):
+            for unused in range(count):
+                if not pending or pending[0][0] not in ready:
+                    return
+                unit, s = pending[0]
+                pending.remove((unit, s))
+                finish(unit, s)
+
+        warm = keep.tile([P, 1], F32)
+        nc.scalar.activation(out=warm[:], in_=tiny[:], func=ACT.Ln)
+        nc.scalar.activation(out=log_pi[:], in_=pi_sb[:].rearrange("p h m -> p (h m)"), func=ACT.Ln, bias=tiny[:])
+        take_logs(0)
+        take_logs(1)
+        vcopy = nc.vector.tensor_copy
+        scopy = nc.scalar.copy
+        jp = joint_pool
+        tp = turn_pool
+        lift_samples(0, 0, vcopy, jp)
+        lift_samples(0, 1, vcopy, jp)
+        square(0)
+        quantise_x(0)
+        quantise_xx(0)
+        lift_samples(1, 0, vcopy, jp)
+        lift_samples(1, 1, vcopy, jp)
+        for m in range(MODES):
+            invert(0, m)
+            weigh_mu(0, m)
+        for m in range(MODES):
+            lift_weights(0, 0, m, jp)
+        for m in range(MODES):
+            lift_weights(1, 0, m, jp)
+        square(1)
+        quantise_x(1)
+        quantise_xx(1)
+        quantise_weights(0, 0)
+        sum_mu_sq(0, 0)
+        sum_mu_sq(0, 1)
+        quantise_weights(1, 0)
+        sum_mu_sq(0, 2)
+        sum_mu_sq(0, 3)
+        finish_bias(0)
+        lift_samples(2, 0, None, jp)
+        lift_samples(2, 1, None, jp)
+        for m in range(MODES):
+            invert(1, m)
+            weigh_mu(1, m)
+        multiply_nth(0)
+        lift_weights(0, 1, 0, tp)
+        lift_weights(0, 1, 1, tp)
+        multiply_nth(1)
+        lift_weights(0, 1, 2, tp)
+        lift_weights(0, 1, 3, tp)
+        start_maximum(0, True)
+        copy_samples(2, 0, vcopy)
+        copy_samples(2, 1, vcopy)
+        lift_weights(1, 1, 0, tp)
+        lift_weights(1, 1, 1, tp)
+        multiply_nth(2)
+        square(2)
+        lift_weights(1, 1, 2, tp)
+        lift_weights(1, 1, 3, tp)
+        multiply_nth(3)
+        lift_samples(3, 0, scopy, tp)
+        lift_samples(3, 1, scopy, tp)
+        start_maximum(1, True)
+        raise_maximum(0, 2)
+        quantise_x(2)
+        raise_maximum(0, 3)
+        quantise_xx(2)
+        multiply_nth(4)
+        multiply_nth(5)
+
+
+        def act(text):
+            for word in text.split():
+                k, v = word[0], int(word[1:])
+                if k == "U":
+                    turn_sum(v // 10, [v % 10])
+                elif k == "T":
+                    turn_sum(v)
+                elif k == "L":
+                    log_sum(v)
+                elif k == "I":
+                    invert_sum(v)
+                elif k == "W":
+                    weigh(v)
+                elif k == "F":
+                    finish_some(v)
+                elif k == "R":
+                    start_maximum(v, True)
+                elif k == "P":
+                    sum_mu_sq(1, v)
+                elif k == "Q":
+                    quantise_weights(v, 1)
+                elif k == "B":
+                    finish_bias(1)
+                elif k == "S":
+                    square(v)
+                elif k == "X":
+                    quantise_x(v)
+                elif k == "Y":
+                    quantise_xx(v)
+                elif k == "E":
+                    exp_first(v)
+                elif k == "e":
+                    exp_mode(v // 10, v % 10)
+                    add_mode(v // 10, v % 10)
+
+        def step(unit, first=""):
+            following = unit + 1
+            on_scalar = following not in ON_VECTOR
+            if following < UNITS and on_scalar and following > 1:
+                start_maximum(following, True)
+            exp_first(unit)
+            for m in range(1, MODES):
+                subtract(unit, m)
+                act(EVENTS.get((unit, m, 0), ""))
+                multiply_nth(unit * OTHER_MODES + m - 1 + JOINT_BANKS)
+                if following < UNITS:
+                    if m == 1:
+                        if not on_scalar:
+                            start_maximum(following, False)
+                    else:
+                        raise_maximum(following, m)
+                        act(EVENTS.get((unit, m, 1), ""))
+                exp_mode(unit, m)
+                add_mode(unit, m)
+                act(EVENTS.get((unit, m, 2), ""))
+
+        for unit in range(UNITS):
+            step(unit)
+        act(TAIL)
+        finish_some(len(pending))

@@ -39,13 +39,14 @@ SCORE_BUFS = 8
 SUM_BUFS = 7
 WEIGHT_BUFS = 8
 RESULT_BUFS = 8
-EVENTS = {(0,1,0): "P0", (0,2,0): "P1", (0,2,1): "P2", (0,3,0): "P3", (0,3,1): "S3", (0,3,2): "X3 Y3", (1,1,0): "Q0", (1,2,0): "Q1 B0", (4,1,0): "T0", (4,2,0): "T1", (4,3,2): "L0 T2 L1 T3 L2 L3 I0 I1 I2 I3", (6,2,1): "W0", (6,3,0): "W1", (6,3,1): "W2", (7,1,0): "W3"}
-TAIL = "F6 U60 F1 T4 L4 U61 F1 U62 F1 U63 L6 T5 L5 F1 T7 L7 F6 I4 W4 I5 W5 I6 W6 I7 W7"
+EVENTS = {(4,1,0): "T0", (4,2,0): "T1", (4,3,2): "L0 T2 L1 T3 L2 L3 I0 W0 I1 W1 I2 W2 I3 W3"}
+TAIL = "F8 U60 F1 T4 L4 U61 F1 U62 F1 U63 L6 T5 L5 F4 I4 W4 I5 W5 I6 W6 F1 T7 L7 I7 W7"
 ON_VECTOR = (6,7)
 TENSOR_SUMS = (6,)
-WEIGH_ON_VECTOR = (0,1,2,3,4)
-LATE_EXP = ()
+WEIGH_ON_VECTOR = ()
 ON_GPSIMD = ()
+RELU_AT = 3
+FIRST = "P0 P1 Q0 P2 P3 S3 B0 Q1 X3 Y3"
 
 
 def tile_dota_mix_pa_kernel(tc, x, gamma_class, mu, cur_var, pi, out):
@@ -96,9 +97,18 @@ def tile_dota_mix_pa_kernel(tc, x, gamma_class, mu, cur_var, pi, out):
             tiles = slice(c * TILES_PER_CHUNK, (c + 1) * TILES_PER_CHUNK)
             nc.sync.dma_start(out=x_sb[:, tiles, :], in_=x_rows[:, tiles, :])
 
-        nc.sync.dma_start(out=var_sb[:, 0, :], in_=var_rows[:, 0, :])
-        load_samples(0)
-        nc.sync.dma_start(out=var_sb[:, 1, :], in_=var_rows[:, 1, :])
+        def load_tiles(first, last):
+            nc.sync.dma_start(out=x_sb[:, first:last, :], in_=x_rows[:, first:last, :])
+
+        def load_modes(target, rows, h, first, last):
+            cols = slice(first * FEATURES, last * FEATURES)
+            nc.sync.dma_start(out=target[:, h, cols], in_=rows[:, h, cols])
+
+        load_modes(var_sb, var_rows, 0, 0, 2)
+        load_tiles(0, 2)
+        load_modes(var_sb, var_rows, 0, 2, 4)
+        load_tiles(2, 4)
+        load_modes(var_sb, var_rows, 1, 0, 4)
         load_samples(1)
         nc.sync.dma_start(out=mu_sb[:, 0, :], in_=mu_rows[:, 0, :])
         load_samples(2)
@@ -111,12 +121,15 @@ def tile_dota_mix_pa_kernel(tc, x, gamma_class, mu, cur_var, pi, out):
         grouped_w = {}
         mu_iv = {}
 
+        def by_value(row):
+            return row.rearrange("p (q t) -> p t q", t=PACK)
+
         def take_logs(h):
             for m in range(MODES):
                 cols = slice(m * FEATURES, (m + 1) * FEATURES)
                 nc.scalar.activation(
-                    out=iv[:, h, cols],
-                    in_=var_sb[:, h, cols],
+                    out=iv[:, h, cols].rearrange("p (t q) -> p t q", t=PACK),
+                    in_=by_value(var_sb[:, h, cols]),
                     func=ACT.Ln,
                     accum_out=log_det[:, h * MODES + m : h * MODES + m + 1],
                 )
@@ -133,7 +146,7 @@ def tile_dota_mix_pa_kernel(tc, x, gamma_class, mu, cur_var, pi, out):
                     t = c * TILES_PER_CHUNK + TILES_PER_BANK * half + j
                     nc.tensor.transpose(
                         bank[:, (TILES_PER_BANK * u + j) * P : (TILES_PER_BANK * u + j + 1) * P],
-                        x_words[:, t, u * P : (u + 1) * P],
+                        x_words[:, t, u : WORD_HALVES * P : WORD_HALVES],
                         identity[:],
                     )
             lifted[(c, half)] = (bank, words)
@@ -173,7 +186,12 @@ def tile_dota_mix_pa_kernel(tc, x, gamma_class, mu, cur_var, pi, out):
             if m == 0:
                 mu_iv_h = stage.tile([P, MODES * FEATURES], F32, bufs=MU_IV_BUFS)
                 mu_iv[h] = mu_iv_h
-            nc.vector.tensor_tensor(out=mu_iv[h][:, cols], in0=mu_sb[:, h, cols], in1=iv[:, h, cols], op=ALU.mult)
+            nc.vector.tensor_tensor(
+                out=mu_iv[h][:, cols].rearrange("p (t q) -> p t q", t=PACK),
+                in0=by_value(mu_sb[:, h, cols]),
+                in1=iv[:, h, cols].rearrange("p (t q) -> p t q", t=PACK),
+                op=ALU.mult,
+            )
 
         def lift_weights(a, h, m, pool):
             if m == 0:
@@ -183,12 +201,9 @@ def tile_dota_mix_pa_kernel(tc, x, gamma_class, mu, cur_var, pi, out):
             cols = slice(m * FEATURES, (m + 1) * FEATURES)
             source = mu_iv[h][:, cols] if a == 1 else iv[:, h, cols]
             factor = 1.0 if a == 1 else -0.5
-            by_value = source.rearrange("p (u q e) -> p u e q", u=WORD_HALVES, e=2)
             bank = pool.tile([P, BANK], F32)
-            for u in range(WORD_HALVES):
-                for odd in range(2):
-                    t = 2 * u + odd
-                    nc.tensor.transpose(bank[:, t * P : (t + 1) * P], by_value[:, u, odd, :], identity[:])
+            for t in range(PACK):
+                nc.tensor.transpose(bank[:, t * P : (t + 1) * P], source[:, t * P : (t + 1) * P], identity[:])
             nc.scalar.activation(
                 out=view[:, m, :, :],
                 in_=bank[:].rearrange("p (t k) -> p k t", t=PACK),
@@ -203,11 +218,12 @@ def tile_dota_mix_pa_kernel(tc, x, gamma_class, mu, cur_var, pi, out):
 
         def sum_mu_sq(h, m):
             cols = slice(m * FEATURES, (m + 1) * FEATURES)
+            weighed = mu_iv[h][:, cols].rearrange("p (t q) -> p t q", t=PACK)
             nc.vector.scalar_tensor_tensor(
-                out=mu_iv[h][:, cols],
-                in0=mu_sb[:, h, cols],
+                out=weighed,
+                in0=by_value(mu_sb[:, h, cols]),
                 scalar=1.0,
-                in1=mu_iv[h][:, cols],
+                in1=weighed,
                 op0=ALU.mult,
                 op1=ALU.mult,
                 accum_out=mu_sq[:, h * MODES + m : h * MODES + m + 1],
@@ -386,71 +402,6 @@ def tile_dota_mix_pa_kernel(tc, x, gamma_class, mu, cur_var, pi, out):
                 pending.remove((unit, s))
                 finish(unit, s)
 
-        warm = keep.tile([P, 1], F32)
-        nc.scalar.activation(out=warm[:], in_=tiny[:], func=ACT.Ln)
-        nc.scalar.activation(out=log_pi[:], in_=pi_sb[:].rearrange("p h m -> p (h m)"), func=ACT.Ln, bias=tiny[:])
-        take_logs(0)
-        take_logs(1)
-        vcopy = nc.vector.tensor_copy
-        scopy = nc.scalar.copy
-        jp = joint_pool
-        tp = turn_pool
-        lift_samples(0, 0, vcopy, jp)
-        lift_samples(0, 1, vcopy, jp)
-        square(0)
-        quantise_x(0)
-        quantise_xx(0)
-        lift_samples(1, 0, vcopy, jp)
-        lift_samples(1, 1, vcopy, jp)
-        for m in range(MODES):
-            invert(0, m)
-            weigh_mu(0, m)
-        for m in range(MODES):
-            lift_weights(0, 0, m, jp)
-        for m in range(MODES):
-            lift_weights(1, 0, m, jp)
-        square(1)
-        quantise_x(1)
-        quantise_xx(1)
-        quantise_weights(0, 0)
-        sum_mu_sq(0, 0)
-        sum_mu_sq(0, 1)
-        quantise_weights(1, 0)
-        sum_mu_sq(0, 2)
-        sum_mu_sq(0, 3)
-        finish_bias(0)
-        lift_samples(2, 0, None, jp)
-        lift_samples(2, 1, None, jp)
-        for m in range(MODES):
-            invert(1, m)
-            weigh_mu(1, m)
-        multiply_nth(0)
-        lift_weights(0, 1, 0, tp)
-        lift_weights(0, 1, 1, tp)
-        multiply_nth(1)
-        lift_weights(0, 1, 2, tp)
-        lift_weights(0, 1, 3, tp)
-        start_maximum(0, True)
-        copy_samples(2, 0, vcopy)
-        copy_samples(2, 1, vcopy)
-        lift_weights(1, 1, 0, tp)
-        lift_weights(1, 1, 1, tp)
-        multiply_nth(2)
-        square(2)
-        lift_weights(1, 1, 2, tp)
-        lift_weights(1, 1, 3, tp)
-        multiply_nth(3)
-        lift_samples(3, 0, scopy, tp)
-        lift_samples(3, 1, scopy, tp)
-        start_maximum(1, True)
-        raise_maximum(0, 2)
-        quantise_x(2)
-        raise_maximum(0, 3)
-        quantise_xx(2)
-        multiply_nth(4)
-        multiply_nth(5)
-
-
         def act(text):
             for word in text.split():
                 k, v = word[0], int(word[1:])
@@ -486,23 +437,87 @@ def tile_dota_mix_pa_kernel(tc, x, gamma_class, mu, cur_var, pi, out):
                     exp_mode(v // 10, v % 10)
                     add_mode(v // 10, v % 10)
 
+        warm = keep.tile([P, 1], F32)
+        nc.scalar.activation(out=warm[:], in_=tiny[:], func=ACT.Ln)
+        nc.scalar.activation(out=log_pi[:], in_=pi_sb[:].rearrange("p h m -> p (h m)"), func=ACT.Ln, bias=tiny[:])
+        take_logs(0)
+        take_logs(1)
+        vcopy = nc.vector.tensor_copy
+        scopy = nc.scalar.copy
+        jp = joint_pool
+        tp = turn_pool
+        lift_samples(0, 0, vcopy, jp)
+        lift_samples(0, 1, vcopy, jp)
+        square(0)
+        quantise_x(0)
+        quantise_xx(0)
+        lift_samples(1, 0, vcopy, jp)
+        lift_samples(1, 1, vcopy, jp)
+        square(1)
+        for m in range(MODES):
+            invert(0, m)
+            weigh_mu(0, m)
+        for m in range(MODES):
+            lift_weights(0, 0, m, jp)
+        for m in range(MODES):
+            lift_weights(1, 0, m, jp)
+        quantise_x(1)
+        quantise_xx(1)
+        quantise_weights(0, 0)
+        sum_mu_sq(0, 0)
+        sum_mu_sq(0, 1)
+        quantise_weights(1, 0)
+        sum_mu_sq(0, 2)
+        sum_mu_sq(0, 3)
+        finish_bias(0)
+        lift_samples(2, 0, None, jp)
+        lift_samples(2, 1, None, jp)
+        for m in range(MODES):
+            invert(1, m)
+            weigh_mu(1, m)
+        multiply_nth(0)
+        lift_weights(0, 1, 0, tp)
+        lift_weights(0, 1, 1, tp)
+        multiply_nth(1)
+        lift_weights(0, 1, 2, tp)
+        lift_weights(0, 1, 3, tp)
+        start_maximum(0, True)
+        copy_samples(2, 0, vcopy)
+        copy_samples(2, 1, vcopy)
+        lift_weights(1, 1, 0, tp)
+        lift_weights(1, 1, 1, tp)
+        multiply_nth(2)
+        square(2)
+        lift_weights(1, 1, 2, tp)
+        lift_weights(1, 1, 3, tp)
+        multiply_nth(3)
+        lift_samples(3, 0, scopy, tp)
+        lift_samples(3, 1, scopy, tp)
+        start_maximum(1, True)
+        quantise_x(2)
+        quantise_xx(2)
+        multiply_nth(4)
+        multiply_nth(5)
+        act(FIRST)
+        raise_maximum(0, 2)
+        raise_maximum(0, 3)
         def step(unit, first=""):
             following = unit + 1
             on_scalar = following not in ON_VECTOR
-            if following < UNITS and on_scalar and following > 1:
-                start_maximum(following, True)
             exp_first(unit)
             for m in range(1, MODES):
-                subtract(unit, m)
-                act(EVENTS.get((unit, m, 0), ""))
-                multiply_nth(unit * OTHER_MODES + m - 1 + JOINT_BANKS)
                 if following < UNITS:
                     if m == 1:
                         if not on_scalar:
                             start_maximum(following, False)
                     else:
                         raise_maximum(following, m)
-                        act(EVENTS.get((unit, m, 1), ""))
+                act(EVENTS.get((unit, m, 1), ""))
+                subtract(unit, m)
+                act(EVENTS.get((unit, m, 0), ""))
+                multiply_nth(unit * OTHER_MODES + m - 1 + JOINT_BANKS)
+                if m == RELU_AT and unit + 2 < UNITS and unit + 2 not in ON_VECTOR:
+                    start_maximum(unit + 2, True)
                 exp_mode(unit, m)
                 add_mode(unit, m)
                 act(EVENTS.get((unit, m, 2), ""))

@@ -46,7 +46,7 @@ TENSOR_SUMS = (6,)
 WEIGH_ON_VECTOR = ()
 ON_GPSIMD = ()
 RELU_AT = 3
-FIRST = "P0 P1 Q0 P2 P3 S3 B0 Q1 X3 Y3"
+FIRST = "m0 h0 h1 w0 w1 m1 w2 w3 h2 h3 R0 C20 C21 S2 l0 l1 m2 l2 l3 M02 X2 M03 Y2 m3 g30 g31 c30 c31 R1 m4 m5 E0 s01 m6 x01 Q0 s02 m7 x02 Q1 s03 m8 x03 q3 P0 P1 P2 P3 B0 X3 M12 M13 Y3 A01 A02 A03 R2"
 
 
 def tile_dota_mix_pa_kernel(tc, x, gamma_class, mu, cur_var, pi, out):
@@ -165,6 +165,11 @@ def tile_dota_mix_pa_kernel(tc, x, gamma_class, mu, cur_var, pi, out):
         def square(c):
             squared_x = stage.tile([P, CHUNK * PACK], BF16, align_bytes=64)
             nc.vector.tensor_tensor(out=squared_x[:], in0=grouped[c][:], in1=grouped[c][:], op=ALU.mult)
+            squared[c] = squared_x
+
+        def square_on_scalar(c):
+            squared_x = stage.tile([P, CHUNK * PACK], BF16, align_bytes=64)
+            nc.scalar.activation(out=squared_x[:], in_=grouped[c][:], func=ACT.Square)
             squared[c] = squared_x
 
         def quantise_samples(c, codes, scales, source):
@@ -433,9 +438,30 @@ def tile_dota_mix_pa_kernel(tc, x, gamma_class, mu, cur_var, pi, out):
                     quantise_xx(v)
                 elif k == "E":
                     exp_first(v)
-                elif k == "e":
+                elif k == "s":
+                    subtract(v // 10, v % 10)
+                elif k == "x":
                     exp_mode(v // 10, v % 10)
+                elif k == "A":
                     add_mode(v // 10, v % 10)
+                elif k == "M":
+                    raise_maximum(v // 10, v % 10)
+                elif k == "m":
+                    multiply_nth(v)
+                elif k == "q":
+                    square_on_scalar(v)
+                elif k == "C":
+                    copy_samples(v // 10, v % 10, vcopy)
+                elif k == "c":
+                    copy_samples(v // 10, v % 10, scopy)
+                elif k == "l":
+                    lift_weights(1, 1, v, tp)
+                elif k == "g":
+                    lift_samples(v // 10, v % 10, None, tp)
+                elif k == "w":
+                    weigh_mu(1, v)
+                elif k == "h":
+                    lift_weights(0, 1, v, tp)
 
         warm = keep.tile([P, 1], F32)
         nc.scalar.activation(out=warm[:], in_=tiny[:], func=ACT.Ln)
@@ -474,33 +500,8 @@ def tile_dota_mix_pa_kernel(tc, x, gamma_class, mu, cur_var, pi, out):
         lift_samples(2, 1, None, jp)
         for m in range(MODES):
             invert(1, m)
-            weigh_mu(1, m)
-        multiply_nth(0)
-        lift_weights(0, 1, 0, tp)
-        lift_weights(0, 1, 1, tp)
-        multiply_nth(1)
-        lift_weights(0, 1, 2, tp)
-        lift_weights(0, 1, 3, tp)
-        start_maximum(0, True)
-        copy_samples(2, 0, vcopy)
-        copy_samples(2, 1, vcopy)
-        lift_weights(1, 1, 0, tp)
-        lift_weights(1, 1, 1, tp)
-        multiply_nth(2)
-        square(2)
-        lift_weights(1, 1, 2, tp)
-        lift_weights(1, 1, 3, tp)
-        multiply_nth(3)
-        lift_samples(3, 0, scopy, tp)
-        lift_samples(3, 1, scopy, tp)
-        start_maximum(1, True)
-        quantise_x(2)
-        quantise_xx(2)
-        multiply_nth(4)
-        multiply_nth(5)
         act(FIRST)
-        raise_maximum(0, 2)
-        raise_maximum(0, 3)
+
         def step(unit, first=""):
             following = unit + 1
             on_scalar = following not in ON_VECTOR
@@ -522,7 +523,7 @@ def tile_dota_mix_pa_kernel(tc, x, gamma_class, mu, cur_var, pi, out):
                 add_mode(unit, m)
                 act(EVENTS.get((unit, m, 2), ""))
 
-        for unit in range(UNITS):
+        for unit in range(1, UNITS):
             step(unit)
         act(TAIL)
         finish_some(len(pending))

@@ -40,13 +40,14 @@ SUM_BUFS = 7
 WEIGHT_BUFS = 8
 RESULT_BUFS = 8
 EVENTS = {(4,1,0): "T0", (4,2,0): "T1", (4,3,2): "L0 T2 L1 T3 L2 L3 I0 W0 I1 W1 I2 W2 I3 W3"}
-TAIL = "F8 U60 F1 T4 L4 U61 F1 U62 F1 U63 L6 T5 L5 F4 I4 W4 I5 W5 I6 W6 F1 T7 L7 I7 W7"
+TAIL = "F8 U60 F1 T4 L4 I4 W4 U61 F1 U62 F1 U63 F4 T5 L5 I5 W5 L6 I6 W6 F4 T7 L7 I7 W7"
 ON_VECTOR = (6,7)
 TENSOR_SUMS = (6,)
 WEIGH_ON_VECTOR = ()
 ON_GPSIMD = ()
 RELU_AT = 3
-FIRST = "m0 h0 h1 w0 w1 m1 w2 w3 h2 h3 R0 C20 C21 S2 l0 l1 m2 l2 l3 M02 X2 M03 Y2 m3 g30 g31 c30 c31 R1 m4 m5 E0 s01 m6 x01 Q0 s02 m7 x02 Q1 s03 m8 x03 q3 P0 P1 P2 P3 B0 X3 M12 M13 Y3 A01 A02 A03 R2"
+LATE_ADDS = ()
+FIRST = "m1 h0 h1 w0 w1 m1 w2 w3 h2 h3 R0 C20 C21 S2 l0 l1 m1 l2 l3 M02 X2 M03 Y2 m1 g30 g31 c30 c31 R1 m2 E0 s01 m1 x01 Q0 s02 m1 x02 Q1 s03 m1 x03 q3 P0 P1 P2 P3 B0 X3 M12 M13 Y3 A01 A02 A03 R2"
 
 
 def tile_dota_mix_pa_kernel(tc, x, gamma_class, mu, cur_var, pi, out):
@@ -261,10 +262,10 @@ def tile_dota_mix_pa_kernel(tc, x, gamma_class, mu, cur_var, pi, out):
             column = (unit // CHUNKS) * MODES + m
             return bias_gap[:, column : column + 1]
 
-        def multiply(unit, m):
+        def multiply(unit, m, pool):
             h, c = divmod(unit, CHUNKS)
             cols = slice(c * CHUNK, (c + 1) * CHUNK)
-            bank = joint_pool.tile([P, BANK], F32)
+            bank = pool.tile([P, BANK], F32)
             passes = [(mode, a) for mode in (m, 0) for a in range(2)]
             for i, (mode, a) in enumerate(passes):
                 classes = slice(mode * P, (mode + 1) * P)
@@ -280,9 +281,21 @@ def tile_dota_mix_pa_kernel(tc, x, gamma_class, mu, cur_var, pi, out):
                 )
             joint[(unit, m)] = bank
 
-        def multiply_nth(n):
-            if n < UNITS * OTHER_MODES:
-                multiply(n // OTHER_MODES, n % OTHER_MODES + 1)
+        groups = [(unit, m) for unit in range(UNITS) for m in range(1, MODES)]
+        in_turn_pool = set()
+
+        def multiply_next(count=1, pool=joint_pool):
+            for unused in range(count):
+                if groups:
+                    group = groups[0]
+                    groups.remove(group)
+                    if pool is turn_pool:
+                        in_turn_pool.add(group)
+                    multiply(group[0], group[1], pool)
+
+        def refill(unit, m):
+            if (unit, m) not in in_turn_pool:
+                multiply_next()
 
         def start_maximum(unit, on_scalar):
             top = work.tile([P, CHUNK], F32)
@@ -333,7 +346,7 @@ def tile_dota_mix_pa_kernel(tc, x, gamma_class, mu, cur_var, pi, out):
 
         def turn_sum(unit, blocks=range(TILES_PER_CHUNK)):
             if unit not in turned:
-                pool = joint_pool if unit in TENSOR_SUMS else turn_pool
+                pool = joint_pool if unit in TENSOR_SUMS and unit > 0 else turn_pool
                 bank = pool.tile([P, BANK], F32)
                 turned[unit] = bank
             bank = turned[unit]
@@ -355,12 +368,14 @@ def tile_dota_mix_pa_kernel(tc, x, gamma_class, mu, cur_var, pi, out):
             bank = turned[unit]
             weight = work.tile([P, TILES_PER_CHUNK, P], F32, bufs=WEIGHT_BUFS)
             nc.scalar.activation(
-                out=weight[:], in_=bank[:].rearrange("p (s k) -> p s k", s=TILES_PER_CHUNK), func=ACT.Ln
+                out=weight[:],
+                in_=bank[:].rearrange("p (s k) -> p s k", s=TILES_PER_CHUNK),
+                func=ACT.Abs_reciprocal_sqrt,
             )
             weights[unit] = weight
 
         def invert_sum(unit):
-            nc.scalar.activation(out=weights[unit][:], in_=weights[unit][:], func=ACT.Exp, scale=-1.0)
+            nc.scalar.activation(out=weights[unit][:], in_=weights[unit][:], func=ACT.Square)
 
         def weigh(unit):
             ready.append(unit)
@@ -447,7 +462,9 @@ def tile_dota_mix_pa_kernel(tc, x, gamma_class, mu, cur_var, pi, out):
                 elif k == "M":
                     raise_maximum(v // 10, v % 10)
                 elif k == "m":
-                    multiply_nth(v)
+                    multiply_next(v)
+                elif k == "n":
+                    multiply_next(v, turn_pool)
                 elif k == "q":
                     square_on_scalar(v)
                 elif k == "C":
@@ -516,11 +533,12 @@ def tile_dota_mix_pa_kernel(tc, x, gamma_class, mu, cur_var, pi, out):
                 act(EVENTS.get((unit, m, 1), ""))
                 subtract(unit, m)
                 act(EVENTS.get((unit, m, 0), ""))
-                multiply_nth(unit * OTHER_MODES + m - 1 + JOINT_BANKS)
+                refill(unit, m)
                 if m == RELU_AT and unit + 2 < UNITS and unit + 2 not in ON_VECTOR:
                     start_maximum(unit + 2, True)
                 exp_mode(unit, m)
-                add_mode(unit, m)
+                if unit not in LATE_ADDS:
+                    add_mode(unit, m)
                 act(EVENTS.get((unit, m, 2), ""))
 
         for unit in range(1, UNITS):

@@ -39,15 +39,20 @@ SCORE_BUFS = 8
 SUM_BUFS = 7
 WEIGHT_BUFS = 8
 RESULT_BUFS = 8
-EVENTS = {(4,1,0): "T0", (4,2,0): "T1", (4,3,2): "L0 T2 L1 T3 L2 L3 I0 W0 I1 W1 I2 W2 I3 W3"}
-TAIL = "F8 U60 F1 T4 L4 I4 W4 U61 F1 U62 F1 U63 F4 T5 L5 I5 W5 L6 I6 W6 F4 T7 L7 I7 W7"
-ON_VECTOR = (6,7)
+EVENTS = {(4,1,0): "T0", (4,2,0): "T1", (4,3,2): "L0 L1 T2 L2 I0 W0 I1 W1 I2 W2", (5,2,1): "T3 L3 I3 W3"}
+TAIL = "F8 T4 U60 F2 L4 I4 A71 W4 U61 F2 A72 U62 F2 U63 L6 I6 F2 T5 L5 I5 W5 A73 W6 D1 F2 D1 F2 D1 F2 D1 F2 T7 L7 I7 W7 D1 F2 D1 F2 D1 F2 D1"
 TENSOR_SUMS = (6,)
-WEIGH_ON_VECTOR = ()
 ON_GPSIMD = ()
 RELU_AT = 3
-LATE_ADDS = ()
-FIRST = "m1 h0 h1 w0 w1 m1 w2 w3 h2 h3 R0 C20 C21 S2 l0 l1 m1 l2 l3 M02 X2 M03 Y2 m1 g30 g31 c30 c31 R1 m2 E0 s01 m1 x01 Q0 s02 m1 x02 Q1 s03 m1 x03 q3 P0 P1 P2 P3 B0 X3 M12 M13 Y3 A01 A02 A03 R2"
+HOLD = (5,)
+LATE_ADDS = (7,)
+WARM = (4, 1, 2)
+EXP_FROM = 2
+SPLIT_EXP = (4,)
+UNIT_ORDER = ((0, 0), (0, 1), (0, 2), (1, 0), (1, 1), (1, 2), (0, 3), (1, 3))
+WEIGH_ON_VECTOR = ()
+ON_VECTOR = (6,7)
+FIRST = "m1 h0 h1 w0 w1 m1 w2 w3 h2 h3 R0 C20 C21 S2 l0 l1 m1 l2 l3 M02 X2 M03 Y2 m1 g30 g31 c30 c31 R1 m2 E0 s01 m1 x01 Q0 s02 m1 x02 Q1 s03 m1 x03 n2 q3 P0 P1 P2 P3 B0 X3 M12 M13 Y3 A01 A02 A03 R2"
 
 
 def tile_dota_mix_pa_kernel(tc, x, gamma_class, mu, cur_var, pi, out):
@@ -259,11 +264,11 @@ def tile_dota_mix_pa_kernel(tc, x, gamma_class, mu, cur_var, pi, out):
         weights = {}
 
         def bias_of(unit, m):
-            column = (unit // CHUNKS) * MODES + m
+            column = UNIT_ORDER[unit][0] * MODES + m
             return bias_gap[:, column : column + 1]
 
         def multiply(unit, m, pool):
-            h, c = divmod(unit, CHUNKS)
+            h, c = UNIT_ORDER[unit]
             cols = slice(c * CHUNK, (c + 1) * CHUNK)
             bank = pool.tile([P, BANK], F32)
             passes = [(mode, a) for mode in (m, 0) for a in range(2)]
@@ -317,24 +322,45 @@ def tile_dota_mix_pa_kernel(tc, x, gamma_class, mu, cur_var, pi, out):
                 op1=ALU.max,
             )
 
-        def exp_first(unit):
+        def scores_of(unit):
             if unit not in exps:
                 expd = scores.tile([P, MODES, CHUNK], F32)
                 exps[unit] = expd
-            expd = exps[unit]
+            return exps[unit]
+
+        def exp_first(unit):
+            expd = scores_of(unit)
             nc.scalar.activation(out=expd[:, 0, :], in_=tops[unit][:], func=ACT.Exp, scale=-1.0)
 
         def subtract(unit, m):
-            expd = exps[unit]
-            nc.vector.tensor_tensor(out=expd[:, m, :], in0=joint[(unit, m)][:], in1=tops[unit][:], op=ALU.subtract)
+            expd = scores_of(unit)
+            nc.vector.scalar_tensor_tensor(
+                out=expd[:, m, :],
+                in0=joint[(unit, m)][:],
+                scalar=bias_of(unit, m),
+                in1=tops[unit][:],
+                op0=ALU.add,
+                op1=ALU.subtract,
+            )
 
         def exp_mode(unit, m):
             expd = exps[unit]
-            nc.scalar.activation(out=expd[:, m, :], in_=expd[:, m, :], func=ACT.Exp, bias=bias_of(unit, m))
+            if m == MODES - 1 and unit not in SPLIT_EXP:
+                nc.scalar.activation(out=expd[:, EXP_FROM:, :], in_=expd[:, EXP_FROM:, :], func=ACT.Exp)
+            elif m < EXP_FROM or unit in SPLIT_EXP:
+                nc.scalar.activation(out=expd[:, m, :], in_=expd[:, m, :], func=ACT.Exp)
 
         def add_mode(unit, m):
             if unit in TENSOR_SUMS:
                 return
+            if m < MODES - 1 and m >= EXP_FROM and unit not in SPLIT_EXP and unit > 0 and unit not in LATE_ADDS:
+                return
+            if m == MODES - 1 and unit not in SPLIT_EXP and unit > 0 and unit not in LATE_ADDS:
+                for other in range(EXP_FROM, MODES - 1):
+                    add_one(unit, other)
+            add_one(unit, m)
+
+        def add_one(unit, m):
             expd = exps[unit]
             if m == 1:
                 total = work.tile([P, CHUNK], F32, bufs=SUM_BUFS)
@@ -346,8 +372,7 @@ def tile_dota_mix_pa_kernel(tc, x, gamma_class, mu, cur_var, pi, out):
 
         def turn_sum(unit, blocks=range(TILES_PER_CHUNK)):
             if unit not in turned:
-                pool = joint_pool if unit in TENSOR_SUMS and unit > 0 else turn_pool
-                bank = pool.tile([P, BANK], F32)
+                bank = turn_pool.tile([P, BANK], F32)
                 turned[unit] = bank
             bank = turned[unit]
             for s in blocks:
@@ -374,12 +399,20 @@ def tile_dota_mix_pa_kernel(tc, x, gamma_class, mu, cur_var, pi, out):
             )
             weights[unit] = weight
 
+        def keep_warm():
+            bank = turn_pool.tile([P, BANK], F32)
+            nc.tensor.matmul(bank[:, :P], lhsT=identity[:], rhs=identity[:], start=True, stop=True)
+
+        def keep_warm_early():
+            bank = joint_pool.tile([P, BANK], F32)
+            nc.tensor.matmul(bank[:, :P], lhsT=identity[:], rhs=identity[:], start=True, stop=True)
+
         def invert_sum(unit):
             nc.scalar.activation(out=weights[unit][:], in_=weights[unit][:], func=ACT.Square)
 
         def weigh(unit):
             ready.append(unit)
-            h, c = divmod(unit, CHUNKS)
+            h, c = UNIT_ORDER[unit]
             tiles = slice(c * TILES_PER_CHUNK, (c + 1) * TILES_PER_CHUNK)
             engine = nc.vector if unit in WEIGH_ON_VECTOR else nc.gpsimd
             engine.tensor_tensor(
@@ -387,7 +420,7 @@ def tile_dota_mix_pa_kernel(tc, x, gamma_class, mu, cur_var, pi, out):
             )
 
         def finish(unit, s):
-            h, c = divmod(unit, CHUNKS)
+            h, c = UNIT_ORDER[unit]
             block = slice(s * P, (s + 1) * P)
             pool = joint_pool if (UNITS - 1, MODES - 1) in joint else turn_pool
             bank = pool.tile([P, BANK], F32)
@@ -429,6 +462,9 @@ def tile_dota_mix_pa_kernel(tc, x, gamma_class, mu, cur_var, pi, out):
                     turn_sum(v // 10, [v % 10])
                 elif k == "T":
                     turn_sum(v)
+                elif k == "D":
+                    for unused in range(v):
+                        keep_warm()
                 elif k == "L":
                     log_sum(v)
                 elif k == "I":
@@ -497,13 +533,17 @@ def tile_dota_mix_pa_kernel(tc, x, gamma_class, mu, cur_var, pi, out):
         lift_samples(1, 0, vcopy, jp)
         lift_samples(1, 1, vcopy, jp)
         square(1)
+        for unused in range(WARM[0]):
+            keep_warm()
         for m in range(MODES):
             invert(0, m)
             weigh_mu(0, m)
-        for m in range(MODES):
-            lift_weights(0, 0, m, jp)
-        for m in range(MODES):
-            lift_weights(1, 0, m, jp)
+        for a in range(2):
+            for m in range(MODES):
+                lift_weights(a, 0, m, jp)
+                if m % 2 == 1:
+                    for unused in range(WARM[1]):
+                        keep_warm()
         quantise_x(1)
         quantise_xx(1)
         quantise_weights(0, 0)
@@ -515,6 +555,8 @@ def tile_dota_mix_pa_kernel(tc, x, gamma_class, mu, cur_var, pi, out):
         finish_bias(0)
         lift_samples(2, 0, None, jp)
         lift_samples(2, 1, None, jp)
+        for unused in range(WARM[2]):
+            keep_warm()
         for m in range(MODES):
             invert(1, m)
         act(FIRST)
@@ -522,7 +564,9 @@ def tile_dota_mix_pa_kernel(tc, x, gamma_class, mu, cur_var, pi, out):
         def step(unit, first=""):
             following = unit + 1
             on_scalar = following not in ON_VECTOR
-            exp_first(unit)
+            held = unit in HOLD
+            if not held:
+                exp_first(unit)
             for m in range(1, MODES):
                 if following < UNITS:
                     if m == 1:
@@ -531,14 +575,20 @@ def tile_dota_mix_pa_kernel(tc, x, gamma_class, mu, cur_var, pi, out):
                     else:
                         raise_maximum(following, m)
                 act(EVENTS.get((unit, m, 1), ""))
+                if held and m == 2:
+                    exp_first(unit)
+                    exp_mode(unit, 1)
+                    if unit not in LATE_ADDS:
+                        add_mode(unit, 1)
                 subtract(unit, m)
                 act(EVENTS.get((unit, m, 0), ""))
                 refill(unit, m)
                 if m == RELU_AT and unit + 2 < UNITS and unit + 2 not in ON_VECTOR:
                     start_maximum(unit + 2, True)
-                exp_mode(unit, m)
-                if unit not in LATE_ADDS:
-                    add_mode(unit, m)
+                if not (held and m == 1):
+                    exp_mode(unit, m)
+                    if unit not in LATE_ADDS:
+                        add_mode(unit, m)
                 act(EVENTS.get((unit, m, 2), ""))
 
         for unit in range(1, UNITS):

from contextlib import ExitStack

import concourse.masks as masks
import concourse.mybir as mybir

F32 = mybir.dt.float32
BF16 = mybir.dt.bfloat16
U32 = mybir.dt.uint32
U8 = mybir.dt.uint8
FP8X4 = mybir.dt.float8_e4m3fn_x4
ACT = mybir.ActivationFunctionType
ALU = mybir.AluOpType

P = 128
SAMPLES, CLASSES, MODES, FEATURES = 2048, 256, 4, 512
PACK = 4
PSUM_BANKS = 8
BANK = 512
ROW_TILES = SAMPLES // P
HALVES = CLASSES // P
CHUNK = BANK
CHUNKS = SAMPLES // CHUNK
TILES_PER_CHUNK = CHUNK // P
WORD_HALVES = FEATURES // 2 // P
TILES_PER_BANK = BANK // (WORD_HALVES * P)
SAMPLES_PER_BANK = TILES_PER_BANK * P
UNITS = HALVES * CHUNKS
OTHER_MODES = MODES - 1
JOINT_BANKS = 6
TURN_BANKS = PSUM_BANKS - JOINT_BANKS
FIRST_ROUND = 5
TINY = 1e-10

FLOPS = 2 * 2 * SAMPLES * CLASSES * MODES * FEATURES


MU_IV_BUFS = 1
SCORE_BUFS = 8
SUM_BUFS = 7
WEIGHT_BUFS = 8
RESULT_BUFS = 8
EVENTS = {(4,1,0): "T0", (4,2,0): "T1", (4,3,2): "L0 L1 T2 L2 I0 W0 I1 W1 I2 W2", (5,2,1): "T3 L3 I3 W3"}
TAIL = "F8 T4 U60 F2 L4 I4 A71 W4 U61 F2 A72 U62 F2 U63 L6 I6 F2 T5 L5 I5 W5 A73 W6 D1 F2 D1 F2 D1 F2 D1 F2 T7 L7 I7 W7 D1 F2 D1 F2 D1 F2 D1"
TENSOR_SUMS = (6,)
ON_GPSIMD = ()
RELU_AT = 3
HOLD = (5,)
LATE_ADDS = (7,)
WARM = (4, 1, 2)
EXP_FROM = 2
SPLIT_EXP = (4,)
UNIT_ORDER = ((0, 0), (0, 1), (0, 2), (1, 0), (1, 1), (1, 2), (0, 3), (1, 3))
WEIGH_ON_VECTOR = ()
ON_VECTOR = (6,7)
FIRST = "m1 h0 h1 w0 w1 m1 w2 w3 h2 h3 R0 C20 C21 S2 l0 l1 m1 l2 l3 M02 X2 M03 Y2 m1 g30 g31 c30 c31 R1 m2 E0 s01 m1 x01 Q0 s02 m1 x02 Q1 s03 m1 x03 n2 q3 P0 P1 P2 P3 B0 X3 M12 M13 Y3 A01 A02 A03 R2"


def tile_dota_mix_pa_kernel(tc, x, gamma_class, mu, cur_var, pi, out):
    nc = tc.nc

    x_rows = x.rearrange("(p t) d -> p t d", t=ROW_TILES)
    gamma_rows = gamma_class.rearrange("(p t) k -> p t k", t=ROW_TILES)
    out_rows = out.rearrange("(p t) k m -> p t (k m)", t=ROW_TILES)
    var_rows = cur_var.rearrange("(h p) m d -> p h (m d)", p=P)
    mu_rows = mu.rearrange("(h p) m d -> p h (m d)", p=P)
    pi_rows = pi.rearrange("(h p) m -> p h m", p=P)

    with ExitStack() as ctx:
        ctx.enter_context(tc.manual_schedule())
        keep = ctx.enter_context(tc.tile_pool(name="keep", bufs=1))
        stage = ctx.enter_context(tc.tile_pool(name="stage", bufs=2))
        scores = ctx.enter_context(tc.tile_pool(name="scores", bufs=SCORE_BUFS))
        work = ctx.enter_context(tc.tile_pool(name="work", bufs=3))
        joint_pool = ctx.enter_context(tc.psum_pool(name="joint", bufs=JOINT_BANKS))
        turn_pool = ctx.enter_context(tc.psum_pool(name="turn", bufs=TURN_BANKS))

        identity = keep.tile([P, P], F32)
        masks.make_identity(nc, identity[:])
        tiny = keep.tile([P, 1], F32)
        nc.vector.memset(tiny[:], TINY)

        x_codes = keep.tile([P, SAMPLES], U32, align_bytes=64)
        x_scales = keep.tile([P, SAMPLES], U8, align_bytes=64)
        xx_codes = keep.tile([P, SAMPLES], U32, align_bytes=64)
        xx_scales = keep.tile([P, SAMPLES], U8, align_bytes=64)
        w_codes = keep.tile([P, 2, HALVES, MODES * P], U32, align_bytes=64)
        w_scales = keep.tile([P, 2, HALVES, MODES * P], U8, align_bytes=64)
        pi_sb = keep.tile([P, HALVES, MODES], BF16)
        log_pi = keep.tile([P, HALVES * MODES], F32)
        log_det = keep.tile([P, HALVES * MODES], F32)
        mu_sq = keep.tile([P, HALVES * MODES], F32)
        bias = keep.tile([P, HALVES * MODES], F32)
        bias_gap = keep.tile([P, HALVES * MODES], F32)
        var_sb = keep.tile([P, HALVES, MODES * FEATURES], BF16)
        mu_sb = keep.tile([P, HALVES, MODES * FEATURES], BF16)
        x_sb = keep.tile([P, ROW_TILES, FEATURES], BF16)
        gamma_sb = keep.tile([P, ROW_TILES, CLASSES], BF16)
        iv = keep.tile([P, HALVES, MODES * FEATURES], F32)

        nc.scalar.dma_start(out=pi_sb[:], in_=pi_rows)

        def load_samples(c):
            tiles = slice(c * TILES_PER_CHUNK, (c + 1) * TILES_PER_CHUNK)
            nc.sync.dma_start(out=x_sb[:, tiles, :], in_=x_rows[:, tiles, :])

        def load_tiles(first, last):
            nc.sync.dma_start(out=x_sb[:, first:last, :], in_=x_rows[:, first:last, :])

        def load_modes(target, rows, h, first, last):
            cols = slice(first * FEATURES, last * FEATURES)
            nc.sync.dma_start(out=target[:, h, cols], in_=rows[:, h, cols])

        load_modes(var_sb, var_rows, 0, 0, 2)
        load_tiles(0, 2)
        load_modes(var_sb, var_rows, 0, 2, 4)
        load_tiles(2, 4)
        load_modes(var_sb, var_rows, 1, 0, 4)
        load_samples(1)
        nc.sync.dma_start(out=mu_sb[:, 0, :], in_=mu_rows[:, 0, :])
        load_samples(2)
        nc.sync.dma_start(out=mu_sb[:, 1, :], in_=mu_rows[:, 1, :])
        load_samples(3)
        nc.sync.dma_start(out=gamma_sb[:], in_=gamma_rows)

        grouped = {}
        squared = {}
        grouped_w = {}
        mu_iv = {}

        def by_value(row):
            return row.rearrange("p (q t) -> p t q", t=PACK)

        def take_logs(h):
            for m in range(MODES):
                cols = slice(m * FEATURES, (m + 1) * FEATURES)
                nc.scalar.activation(
                    out=iv[:, h, cols].rearrange("p (t q) -> p t q", t=PACK),
                    in_=by_value(var_sb[:, h, cols]),
                    func=ACT.Ln,
                    accum_out=log_det[:, h * MODES + m : h * MODES + m + 1],
                )

        def lift_samples(c, half, copy, pool):
            x_words = x_sb[:].bitcast(F32)
            if half == 0:
                grouped_x = stage.tile([P, CHUNK * PACK], BF16, align_bytes=64)
                grouped[c] = grouped_x
            words = grouped[c][:].bitcast(F32).rearrange("p (b u) -> p b u", u=WORD_HALVES)
            bank = pool.tile([P, BANK], F32)
            for u in range(WORD_HALVES):
                for j in range(TILES_PER_BANK):
                    t = c * TILES_PER_CHUNK + TILES_PER_BANK * half + j
                    nc.tensor.transpose(
                        bank[:, (TILES_PER_BANK * u + j) * P : (TILES_PER_BANK * u + j + 1) * P],
                        x_words[:, t, u : WORD_HALVES * P : WORD_HALVES],
                        identity[:],
                    )
            lifted[(c, half)] = (bank, words)
            if copy:
                copy_samples(c, half, copy)

        lifted = {}

        def copy_samples(c, half, copy):
            bank, words = lifted[(c, half)]
            copy(
                out=words[:, half * SAMPLES_PER_BANK : (half + 1) * SAMPLES_PER_BANK, :],
                in_=bank[:].rearrange("p (u b) -> p b u", u=WORD_HALVES),
            )

        def square(c):
            squared_x = stage.tile([P, CHUNK * PACK], BF16, align_bytes=64)
            nc.vector.tensor_tensor(out=squared_x[:], in0=grouped[c][:], in1=grouped[c][:], op=ALU.mult)
            squared[c] = squared_x

        def square_on_scalar(c):
            squared_x = stage.tile([P, CHUNK * PACK], BF16, align_bytes=64)
            nc.scalar.activation(out=squared_x[:], in_=grouped[c][:], func=ACT.Square)
            squared[c] = squared_x

        def quantise_samples(c, codes, scales, source):
            cols = slice(c * CHUNK, (c + 1) * CHUNK)
            nc.vector.quantize_mx(out=codes[:, cols].bitcast(FP8X4), scales=scales[:, cols], in_=source[c][:])

        def quantise_x(c):
            quantise_samples(c, x_codes, x_scales, grouped)

        def quantise_xx(c):
            quantise_samples(c, xx_codes, xx_scales, squared)

        def invert(h, m):
            cols = slice(m * FEATURES, (m + 1) * FEATURES)
            nc.scalar.activation(out=iv[:, h, cols], in_=iv[:, h, cols], func=ACT.Exp, scale=-1.0)

        def weigh_mu(h, m):
            cols = slice(m * FEATURES, (m + 1) * FEATURES)
            if m == 0:
                mu_iv_h = stage.tile([P, MODES * FEATURES], F32, bufs=MU_IV_BUFS)
                mu_iv[h] = mu_iv_h
            nc.vector.tensor_tensor(
                out=mu_iv[h][:, cols].rearrange("p (t q) -> p t q", t=PACK),
                in0=by_value(mu_sb[:, h, cols]),
                in1=iv[:, h, cols].rearrange("p (t q) -> p t q", t=PACK),
                op=ALU.mult,
            )

        def lift_weights(a, h, m, pool):
            if m == 0:
                grouped_wa = stage.tile([P, MODES * P * PACK], BF16, align_bytes=64, bufs=2)
                grouped_w[(a, h)] = grouped_wa
            view = grouped_w[(a, h)][:].rearrange("p (m k t) -> p m k t", m=MODES, t=PACK)
            cols = slice(m * FEATURES, (m + 1) * FEATURES)
            source = mu_iv[h][:, cols] if a == 1 else iv[:, h, cols]
            factor = 1.0 if a == 1 else -0.5
            bank = pool.tile([P, BANK], F32)
            for t in range(PACK):
                nc.tensor.transpose(bank[:, t * P : (t + 1) * P], source[:, t * P : (t + 1) * P], identity[:])
            nc.scalar.activation(
                out=view[:, m, :, :],
                in_=bank[:].rearrange("p (t k) -> p k t", t=PACK),
                func=ACT.Copy,
                scale=factor if m > 0 else -factor,
            )

        def quantise_weights(a, h):
            nc.vector.quantize_mx(
                out=w_codes[:, a, h, :].bitcast(FP8X4), scales=w_scales[:, a, h, :], in_=grouped_w[(a, h)][:]
            )

        def sum_mu_sq(h, m):
            cols = slice(m * FEATURES, (m + 1) * FEATURES)
            weighed = mu_iv[h][:, cols].rearrange("p (t q) -> p t q", t=PACK)
            nc.vector.scalar_tensor_tensor(
                out=weighed,
                in0=by_value(mu_sb[:, h, cols]),
                scalar=1.0,
                in1=weighed,
                op0=ALU.mult,
                op1=ALU.mult,
                accum_out=mu_sq[:, h * MODES + m : h * MODES + m + 1],
            )

        def finish_bias(h):
            modes = slice(h * MODES, (h + 1) * MODES)
            nc.gpsimd.tensor_tensor(out=bias[:, modes], in0=log_det[:, modes], in1=mu_sq[:, modes], op=ALU.add)
            nc.gpsimd.tensor_scalar(
                out=bias[:, modes], in0=bias[:, modes], scalar1=-0.5, scalar2=0.0, op0=ALU.mult, op1=ALU.add
            )
            nc.gpsimd.tensor_tensor(out=bias[:, modes], in0=bias[:, modes], in1=log_pi[:, modes], op=ALU.add)
            nc.gpsimd.tensor_scalar(
                out=bias_gap[:, modes],
                in0=bias[:, modes],
                scalar1=bias[:, h * MODES : h * MODES + 1],
                scalar2=0.0,
                op0=ALU.subtract,
                op1=ALU.add,
            )

        joint = {}
        tops = {}
        exps = {}
        sums = {}
        turned = {}
        weights = {}

        def bias_of(unit, m):
            column = UNIT_ORDER[unit][0] * MODES + m
            return bias_gap[:, column : column + 1]

        def multiply(unit, m, pool):
            h, c = UNIT_ORDER[unit]
            cols = slice(c * CHUNK, (c + 1) * CHUNK)
            bank = pool.tile([P, BANK], F32)
            passes = [(mode, a) for mode in (m, 0) for a in range(2)]
            for i, (mode, a) in enumerate(passes):
                classes = slice(mode * P, (mode + 1) * P)
                moving_codes, moving_scales = ((xx_codes, xx_scales), (x_codes, x_scales))[a]
                nc.tensor.matmul_mx(
                    out=bank[:],
                    lhsT=w_codes[:, a, h, classes].bitcast(FP8X4),
                    lhsT_scale=w_scales[:, a, h, classes],
                    rhs=moving_codes[:, cols].bitcast(FP8X4),
                    rhs_scale=moving_scales[:, cols],
                    start=(i == 0),
                    stop=(i == len(passes) - 1),
                )
            joint[(unit, m)] = bank

        groups = [(unit, m) for unit in range(UNITS) for m in range(1, MODES)]
        in_turn_pool = set()

        def multiply_next(count=1, pool=joint_pool):
            for unused in range(count):
                if groups:
                    group = groups[0]
                    groups.remove(group)
                    if pool is turn_pool:
                        in_turn_pool.add(group)
                    multiply(group[0], group[1], pool)

        def refill(unit, m):
            if (unit, m) not in in_turn_pool:
                multiply_next()

        def start_maximum(unit, on_scalar):
            top = work.tile([P, CHUNK], F32)
            tops[unit] = top
            if on_scalar:
                nc.scalar.activation(out=top[:], in_=joint[(unit, 1)][:], func=ACT.Relu, bias=bias_of(unit, 1))
            else:
                nc.vector.tensor_scalar(
                    out=top[:], in0=joint[(unit, 1)][:], scalar1=bias_of(unit, 1), scalar2=0.0, op0=ALU.add, op1=ALU.max
                )

        def raise_maximum(unit, m):
            nc.vector.scalar_tensor_tensor(
                out=tops[unit][:],
                in0=joint[(unit, m)][:],
                scalar=bias_of(unit, m),
                in1=tops[unit][:],
                op0=ALU.add,
                op1=ALU.max,
            )

        def scores_of(unit):
            if unit not in exps:
                expd = scores.tile([P, MODES, CHUNK], F32)
                exps[unit] = expd
            return exps[unit]

        def exp_first(unit):
            expd = scores_of(unit)
            nc.scalar.activation(out=expd[:, 0, :], in_=tops[unit][:], func=ACT.Exp, scale=-1.0)

        def subtract(unit, m):
            expd = scores_of(unit)
            nc.vector.scalar_tensor_tensor(
                out=expd[:, m, :],
                in0=joint[(unit, m)][:],
                scalar=bias_of(unit, m),
                in1=tops[unit][:],
                op0=ALU.add,
                op1=ALU.subtract,
            )

        def exp_mode(unit, m):
            expd = exps[unit]
            if m == MODES - 1 and unit not in SPLIT_EXP:
                nc.scalar.activation(out=expd[:, EXP_FROM:, :], in_=expd[:, EXP_FROM:, :], func=ACT.Exp)
            elif m < EXP_FROM or unit in SPLIT_EXP:
                nc.scalar.activation(out=expd[:, m, :], in_=expd[:, m, :], func=ACT.Exp)

        def add_mode(unit, m):
            if unit in TENSOR_SUMS:
                return
            if m < MODES - 1 and m >= EXP_FROM and unit not in SPLIT_EXP and unit > 0 and unit not in LATE_ADDS:
                return
            if m == MODES - 1 and unit not in SPLIT_EXP and unit > 0 and unit not in LATE_ADDS:
                for other in range(EXP_FROM, MODES - 1):
                    add_one(unit, other)
            add_one(unit, m)

        def add_one(unit, m):
            expd = exps[unit]
            if m == 1:
                total = work.tile([P, CHUNK], F32, bufs=SUM_BUFS)
                sums[unit] = total
            total = sums[unit]
            nc.gpsimd.tensor_tensor(
                out=total[:], in0=expd[:, 0, :] if m == 1 else total[:], in1=expd[:, m, :], op=ALU.add
            )

        def turn_sum(unit, blocks=range(TILES_PER_CHUNK)):
            if unit not in turned:
                bank = turn_pool.tile([P, BANK], F32)
                turned[unit] = bank
            bank = turned[unit]
            for s in blocks:
                block = slice(s * P, (s + 1) * P)
                if unit in TENSOR_SUMS:
                    for m in range(MODES):
                        nc.tensor.matmul(
                            bank[:, block],
                            lhsT=exps[unit][:, m, block],
                            rhs=identity[:],
                            start=(m == 0),
                            stop=(m == MODES - 1),
                        )
                else:
                    nc.tensor.transpose(bank[:, block], sums[unit][:, block], identity[:])

        def log_sum(unit):
            bank = turned[unit]
            weight = work.tile([P, TILES_PER_CHUNK, P], F32, bufs=WEIGHT_BUFS)
            nc.scalar.activation(
                out=weight[:],
                in_=bank[:].rearrange("p (s k) -> p s k", s=TILES_PER_CHUNK),
                func=ACT.Abs_reciprocal_sqrt,
            )
            weights[unit] = weight

        def keep_warm():
            bank = turn_pool.tile([P, BANK], F32)
            nc.tensor.matmul(bank[:, :P], lhsT=identity[:], rhs=identity[:], start=True, stop=True)

        def keep_warm_early():
            bank = joint_pool.tile([P, BANK], F32)
            nc.tensor.matmul(bank[:, :P], lhsT=identity[:], rhs=identity[:], start=True, stop=True)

        def invert_sum(unit):
            nc.scalar.activation(out=weights[unit][:], in_=weights[unit][:], func=ACT.Square)

        def weigh(unit):
            ready.append(unit)
            h, c = UNIT_ORDER[unit]
            tiles = slice(c * TILES_PER_CHUNK, (c + 1) * TILES_PER_CHUNK)
            engine = nc.vector if unit in WEIGH_ON_VECTOR else nc.gpsimd
            engine.tensor_tensor(
                out=weights[unit][:], in0=weights[unit][:], in1=gamma_sb[:, tiles, h * P : (h + 1) * P], op=ALU.mult
            )

        def finish(unit, s):
            h, c = UNIT_ORDER[unit]
            block = slice(s * P, (s + 1) * P)
            pool = joint_pool if (UNITS - 1, MODES - 1) in joint else turn_pool
            bank = pool.tile([P, BANK], F32)
            for m in range(MODES):
                nc.tensor.transpose(bank[:, m * P : (m + 1) * P], exps[unit][:, m, block], identity[:])
            result = work.tile([P, P * MODES], F32, bufs=RESULT_BUFS)
            source = bank
            engine = nc.vector
            if (unit, s) in ON_GPSIMD:
                plain = work.tile([P, P * MODES], F32, bufs=2)
                nc.scalar.copy(out=plain[:], in_=bank[:])
                source = plain
                engine = nc.gpsimd
            engine.tensor_tensor(
                out=result[:].rearrange("p (k m) -> p k m", m=MODES),
                in0=source[:].rearrange("p (m k) -> p k m", m=MODES),
                in1=weights[unit][:, s, :].unsqueeze(2).to_broadcast([P, P, MODES]),
                op=ALU.mult,
            )
            nc.sync.dma_start(
                out=out_rows[:, c * TILES_PER_CHUNK + s, h * P * MODES : (h + 1) * P * MODES], in_=result[:]
            )

        ready = []
        pending = [(unit, s) for unit in range(UNITS) for s in range(TILES_PER_CHUNK)]

        def finish_some(count):
            for unused in range(count):
                if not pending or pending[0][0] not in ready:
                    return
                unit, s = pending[0]
                pending.remove((unit, s))
                finish(unit, s)

        def act(text):
            for word in text.split():
                k, v = word[0], int(word[1:])
                if k == "U":
                    turn_sum(v // 10, [v % 10])
                elif k == "T":
                    turn_sum(v)
                elif k == "D":
                    for unused in range(v):
                        keep_warm()
                elif k == "L":
                    log_sum(v)
                elif k == "I":
                    invert_sum(v)
                elif k == "W":
                    weigh(v)
                elif k == "F":
                    finish_some(v)
                elif k == "R":
                    start_maximum(v, True)
                elif k == "P":
                    sum_mu_sq(1, v)
                elif k == "Q":
                    quantise_weights(v, 1)
                elif k == "B":
                    finish_bias(1)
                elif k == "S":
                    square(v)
                elif k == "X":
                    quantise_x(v)
                elif k == "Y":
                    quantise_xx(v)
                elif k == "E":
                    exp_first(v)
                elif k == "s":
                    subtract(v // 10, v % 10)
                elif k == "x":
                    exp_mode(v // 10, v % 10)
                elif k == "A":
                    add_mode(v // 10, v % 10)
                elif k == "M":
                    raise_maximum(v // 10, v % 10)
                elif k == "m":
                    multiply_next(v)
                elif k == "n":
                    multiply_next(v, turn_pool)
                elif k == "q":
                    square_on_scalar(v)
                elif k == "C":
                    copy_samples(v // 10, v % 10, vcopy)
                elif k == "c":
                    copy_samples(v // 10, v % 10, scopy)
                elif k == "l":
                    lift_weights(1, 1, v, tp)
                elif k == "g":
                    lift_samples(v // 10, v % 10, None, tp)
                elif k == "w":
                    weigh_mu(1, v)
                elif k == "h":
                    lift_weights(0, 1, v, tp)

        warm = keep.tile([P, 1], F32)
        nc.scalar.activation(out=warm[:], in_=tiny[:], func=ACT.Ln)
        nc.scalar.activation(out=log_pi[:], in_=pi_sb[:].rearrange("p h m -> p (h m)"), func=ACT.Ln, bias=tiny[:])
        take_logs(0)
        take_logs(1)
        vcopy = nc.vector.tensor_copy
        scopy = nc.scalar.copy
        jp = joint_pool
        tp = turn_pool
        lift_samples(0, 0, vcopy, jp)
        lift_samples(0, 1, vcopy, jp)
        square(0)
        quantise_x(0)
        quantise_xx(0)
        lift_samples(1, 0, vcopy, jp)
        lift_samples(1, 1, vcopy, jp)
        square(1)
        for unused in range(WARM[0]):
            keep_warm()
        for m in range(MODES):
            invert(0, m)
            weigh_mu(0, m)
        for a in range(2):
            for m in range(MODES):
                lift_weights(a, 0, m, jp)
                if m % 2 == 1:
                    for unused in range(WARM[1]):
                        keep_warm()
        quantise_x(1)
        quantise_xx(1)
        quantise_weights(0, 0)
        sum_mu_sq(0, 0)
        sum_mu_sq(0, 1)
        quantise_weights(1, 0)
        sum_mu_sq(0, 2)
        sum_mu_sq(0, 3)
        finish_bias(0)
        lift_samples(2, 0, None, jp)
        lift_samples(2, 1, None, jp)
        for unused in range(WARM[2]):
            keep_warm()
        for m in range(MODES):
            invert(1, m)
        act(FIRST)

        def step(unit, first=""):
            following = unit + 1
            on_scalar = following not in ON_VECTOR
            held = unit in HOLD
            if not held:
                exp_first(unit)
            for m in range(1, MODES):
                if following < UNITS:
                    if m == 1:
                        if not on_scalar:
                            start_maximum(following, False)
                    else:
                        raise_maximum(following, m)
                act(EVENTS.get((unit, m, 1), ""))
                if held and m == 2:
                    exp_first(unit)
                    exp_mode(unit, 1)
                    if unit not in LATE_ADDS:
                        add_mode(unit, 1)
                subtract(unit, m)
                act(EVENTS.get((unit, m, 0), ""))
                refill(unit, m)
                if m == RELU_AT and unit + 2 < UNITS and unit + 2 not in ON_VECTOR:
                    start_maximum(unit + 2, True)
                if not (held and m == 1):
                    exp_mode(unit, m)
                    if unit not in LATE_ADDS:
                        add_mode(unit, m)
                act(EVENTS.get((unit, m, 2), ""))

        for unit in range(1, UNITS):
            step(unit)
        act(TAIL)
        finish_some(len(pending))
